import numpy as np
import ml_dtypes


def mxq(x, axis, fmt="e4m3"):
    dtype, down = {"e4m3": (ml_dtypes.float8_e4m3fn, 7), "e5m2": (ml_dtypes.float8_e5m2, 14)}[fmt]
    v = np.moveaxis(np.asarray(x, np.float32).astype(ml_dtypes.bfloat16).astype(np.float64), axis, -1)
    blocks = v.reshape(v.shape[:-1] + (-1, 32))
    amax = np.abs(blocks).max(-1, keepdims=True)
    byte = np.maximum(np.where(amax > 0, np.frexp(amax)[1] - 1 + 127, 0) - down, 1)
    scale = np.exp2(byte - 127.0)
    codes = (blocks / scale).astype(np.float32).astype(dtype).astype(np.float64)
    return np.moveaxis((codes * scale).reshape(v.shape), -1, axis)


WIDE = False


def mx_kscale(k):
    if not WIDE:
        return np.ones(k)
    levels = np.array([10, -10, 5, -5, 0])
    if k % 512:
        return np.exp2(np.random.permutation(np.resize(levels, k // 32))).repeat(32)
    a = np.empty((k // 512, 16))
    for p in range(k // 512):
        a[p, :8] = np.random.permutation(np.resize(levels, 8))
        for g in range(8):
            far = levels[np.abs(levels - a[p, g]) >= 10]
            a[p, g + 8] = far[np.random.randint(len(far))]
    return np.exp2(a.ravel()).repeat(32)


BF16 = ml_dtypes.bfloat16


def bf(x):
    return np.asarray(x, np.float32).astype(BF16)


def f64(x):
    return np.asarray(x).astype(np.float64)


B, S, D, H, DH, QB = 1, 1024, 1024, 8, 128, 512
HD = H * DH
ROPE_BASE = 10000.0


def rope(t):
    b, h, s, d = t.shape
    inv_freq = 1.0 / (ROPE_BASE ** (np.arange(0, d, 2) / d))
    ang = np.arange(s)[:, None] * inv_freq[None, :]
    cos = np.cos(ang)[None, None]
    sin = np.sin(ang)[None, None]
    t1 = t[..., 0::2]
    t2 = t[..., 1::2]
    r1 = t1 * cos - t2 * sin
    r2 = t1 * sin + t2 * cos
    return np.stack([r1, r2], axis=-1).reshape(b, h, s, d)


def draw0():
    s = mx_kscale(D)
    return {"x": bf(np.random.standard_normal((B, S, D)) * s),
            "wq": bf(np.random.standard_normal((HD, D)) / np.sqrt(D) / s[None, :]),
            "wk": bf(np.random.standard_normal((HD, D)) / np.sqrt(D) / s[None, :])}


def core(x, wq, wk):
    xq = mxq(f64(x), 2, "e4m3")
    q = (xq @ mxq(f64(wq), 1, "e4m3").T).reshape(B, S, H, DH).transpose(0, 2, 1, 3)
    k = (xq @ mxq(f64(wk), 1, "e4m3").T).reshape(B, S, H, DH).transpose(0, 2, 1, 3)
    return np.maximum(rope(q), 0.0), np.maximum(rope(k), 0.0)


def e4m3fn_bytes(y):
    return np.clip(np.asarray(y, np.float64), -448.0, 448.0).astype(np.float32).astype(ml_dtypes.float8_e4m3fn).view(np.uint8)


def e4m3fn_values(b):
    return np.asarray(b, np.uint8).view(ml_dtypes.float8_e4m3fn).astype(np.float64)


def setup_inputs():
    d = draw0()
    x0 = np.asarray(d['x']).astype(np.float64)
    s = (np.max(np.abs(x0), axis=(0, 1), keepdims=True) / 448.0).astype(np.float32)
    out = {}
    for k, v in d.items():
        if k == 'x':
            out['x_bytes'] = e4m3fn_bytes(x0 / s.astype(np.float64))
            out['x_scale'] = s
        else:
            out[k] = v
    return out


def reference(x_bytes, x_scale, wq, wk):
    return core(e4m3fn_values(x_bytes) * x_scale.astype(np.float64), wq, wk)

@@ -1,0 +1,290 @@
+from contextlib import ExitStack
+import math
+
+import concourse.masks as masks
+import concourse.mybir as mybir
+
+FLOPS = 2 * 1024 * 1024 * 2048
+
+F32 = mybir.dt.float32
+BF16 = mybir.dt.bfloat16
+U32 = mybir.dt.uint32
+U8 = mybir.dt.uint8
+I32 = mybir.dt.int32
+FP8 = mybir.dt.float8_e4m3fn
+FP8X4 = mybir.dt.float8_e4m3fn_x4
+ALU = mybir.AluOpType
+ACT = mybir.ActivationFunctionType
+
+P = 128
+TWO_PI = 2.0 * math.pi
+PLAIN_UNITS = 3
+
+
+def tile_linearattention_pa_kernel(tc, x_bytes, x_scale, wq, wk, out_0, out_1):
+    nc = tc.nc
+    with ExitStack() as ctx:
+        ctx.enter_context(tc.manual_schedule(engines={mybir.EngineType.DVE}))
+        const = ctx.enter_context(tc.tile_pool(name="const", bufs=1))
+        p2 = ctx.enter_context(tc.tile_pool(name="p2", bufs=2))
+        p3 = ctx.enter_context(tc.tile_pool(name="p3", bufs=3))
+        p8 = ctx.enter_context(tc.tile_pool(name="p8", bufs=8))
+        accp = ctx.enter_context(tc.psum_pool(name="accp", bufs=2))
+
+        xv = x_bytes[0].rearrange("(p i) k -> p (i k)", i=8)
+        xby = []
+        for q in range(4):
+            xbq = const.tile([P, 2048], U8, name="xbytes%d" % q)
+            xby.append(xbq)
+        xsc = const.tile([P, 1024], F32, name="xsc")
+        wraw = []
+        for rt in range(16):
+            wr = const.tile([P, 1024], BF16, name="wraw%d" % rt)
+            wraw.append(wr)
+
+        def load_x(q):
+            nc.sync.dma_start(out=xby[q][:], in_=xv[:, 2048 * q:2048 * (q + 1)])
+
+        def load_w(rt):
+            src = wq if rt < 8 else wk
+            r0 = 128 * (rt % 8)
+            nc.sync.dma_start(out=wraw[rt][:], in_=src[r0:r0 + 128, :])
+
+        load_x(0)
+        nc.sync.dma_start(out=xsc[:], in_=x_scale[0].rearrange("o k -> (o k)").partition_broadcast(P))
+        for q in range(1, 4):
+            load_w(2 * q - 2)
+            load_w(2 * q - 1)
+            load_x(q)
+        for rt in range(6, 16):
+            load_w(rt)
+
+        posi = const.tile([P, 8], I32, name="posi")
+        nc.gpsimd.iota(posi[:], pattern=[[1, 8]], base=0, channel_multiplier=8)
+        one = const.tile([P, 1], F32, name="one")
+        nc.vector.memset(one[:], 1.0)
+        warm = const.tile([P, 1], F32, name="warm")
+        nc.scalar.activation(out=warm[:], in_=one[:], func=ACT.Sin)
+
+        ident = const.tile([P, P], F32, name="ident")
+        masks.make_identity(nc, ident[:])
+        perm = const.tile([P, P], F32, name="perm")
+        nc.scalar.copy(out=perm[:, 0:64], in_=ident[:, 1:128:2])
+        nc.scalar.copy(out=perm[:, 64:128], in_=ident[:, 0:128:2])
+
+
+        th = const.tile([P, 1, 64], F32, name="th")
+        thf = th[:].rearrange("p o j -> p (o j)")
+        nc.vector.memset(thf, 1.0)
+        nc.vector.tensor_scalar_mul(out=thf, in0=thf, scalar1=1.0 / TWO_PI)
+        for b in range(6):
+            half = thf.rearrange("p (a two l) -> p a two l", two=2, l=1 << b)[:, :, 1, :]
+            nc.vector.tensor_scalar_mul(out=half, in0=half, scalar1=10000.0 ** (-(1 << b) / 64.0))
+
+        posf = const.tile([P, 8, 1], F32, name="posf")
+        nc.vector.tensor_copy(out=posf[:].rearrange("p i o -> p (i o)"), in_=posi[:])
+        tau = const.tile([P, 8, 64], F32, name="tau")
+        nc.vector.tensor_tensor(
+            out=tau[:], in0=th[:].to_broadcast([P, 8, 64]), in1=posf[:].to_broadcast([P, 8, 64]), op=ALU.mult
+        )
+        ki = const.tile([P, 8, 64], I32, name="ki")
+        nc.vector.tensor_copy(out=ki[:], in_=tau[:])
+        fr = const.tile([P, 8, 64], F32, name="fr")
+        nc.vector.tensor_tensor(out=fr[:], in0=tau[:], in1=ki[:], op=ALU.subtract)
+        ng = const.tile([P, 8, 64], F32, name="ng")
+        nc.vector.scalar_tensor_tensor(out=ng[:], in0=fr[:], scalar=0.5, in1=fr[:], op0=ALU.is_gt, op1=ALU.subtract)
+        ab = const.tile([P, 8, 64], F32, name="ab")
+        nc.vector.scalar_tensor_tensor(out=ab[:], in0=ng[:], scalar=-1.0, in1=ng[:], op0=ALU.mult, op1=ALU.max)
+
+        ctab = const.tile([P, 8, 1, 1, 64], F32, name="ctab")
+        nc.scalar.activation(
+            out=ctab[:].rearrange("p i a b j -> p i (a b j)"), in_=ab[:], func=ACT.Sin, bias=math.pi / 2.0, scale=-TWO_PI
+        )
+        stab = const.tile([P, 8, 2, 1, 64], F32, name="stab")
+        sview = stab[:].rearrange("p i x o j -> p i x (o j)")
+        nc.scalar.activation(out=sview[:, :, 0, :], in_=ng[:], func=ACT.Sin, scale=TWO_PI)
+        nc.scalar.activation(out=sview[:, :, 1, :], in_=ng[:], func=ACT.Sin, scale=-TWO_PI)
+        ttab = const.tile([P, 8, 2, 1, 64], F32, name="ttab")
+        nc.gpsimd.tensor_tensor(
+            out=ttab[:].rearrange("p i x o j -> p i x (o j)"),
+            in0=sview,
+            in1=ctab[:].rearrange("p i a b j -> p i a (b j)").to_broadcast([P, 8, 2, 64]),
+            op=ALU.subtract,
+        )
+
+        xcodes = const.tile([P, 2048], U32, name="xcodes", align_bytes=64)
+        xscl = const.tile([P, 2048], U8, name="xscl", align_bytes=64)
+        wcodes = const.tile([P, 4096], U32, name="wcodes", align_bytes=64)
+        wscl = const.tile([P, 4096], U8, name="wscl", align_bytes=64)
+
+        def widen(i):
+            xw = p8.tile([P, 1024], BF16, name="xw")
+            lo = 1024 * (i % 2)
+            nc.vector.tensor_tensor(
+                out=xw[:], in0=xby[i // 2][:, lo:lo + 1024].bitcast(FP8), in1=xsc[:], op=ALU.mult
+            )
+            return xw
+
+        def turn(pool, words, eye, u_major):
+            bank = pool.tile([P, 4, P], F32, name="tp")
+            for g in range(2):
+                for u in range(2):
+                    slot = 2 * u + g if u_major else 2 * g + u
+                    nc.tensor.transpose(bank[:, slot, :], words[:, 256 * g + u:256 * (g + 1):2], eye[:])
+            return bank
+
+        xgs = {}
+
+        def turn_x(pool, i, xw):
+            if i % 4 == 0:
+                xg = p2.tile([P, 4096], BF16, name="xg", align_bytes=64)
+                xgs[i // 4] = xg
+            xgw = xgs[i // 4][:].bitcast(F32).rearrange("p (i g r u) -> p i g r u", i=4, g=2, u=2)
+            bank = turn(pool, xw[:].bitcast(F32), ident, False)
+            nc.scalar.copy(out=xgw[:, i % 4], in_=bank[:].rearrange("p (g u) r -> p g r u", u=2))
+
+        def quant_x(q):
+            cols = slice(1024 * q, 1024 * (q + 1))
+            nc.vector.quantize_mx(out=xcodes[:, cols].bitcast(FP8X4), scales=xscl[:, cols], in_=xgs[q][:])
+
+        wgs = {}
+
+        def turn_w(pool, t, h):
+            if h == 0:
+                wg = p2.tile([P, 8192], BF16, name="wg", align_bytes=64)
+                wgs[t] = wg
+            wgw = wgs[t][:].bitcast(F32).rearrange("p (gx h j u) -> p gx h j u", gx=4, h=8, u=2)
+            bank = turn(pool, wraw[8 * t + h][:].bitcast(F32), perm, True)
+            nc.scalar.copy(out=wgw[:, :, h], in_=bank[:].rearrange("p (u g) (x j) -> p u (g x) j", u=2, x=2).rearrange("p u gx j -> p gx j u"))
+
+        def quant_w(t, g):
+            cols = slice(1024 * (2 * t + g), 1024 * (2 * t + g + 1))
+            nc.vector.quantize_mx(
+                out=wcodes[:, cols].bitcast(FP8X4), scales=wscl[:, cols], in_=wgs[t][:, 4096 * g:4096 * (g + 1)]
+            )
+
+        def mx(out, t, i, g, x, start, stop):
+            xs = slice(128 * (2 * i + g), 128 * (2 * i + g + 1))
+            w0 = 1024 * (2 * t + g) + 512 * x
+            nc.tensor.matmul_mx(
+                out=out[:],
+                lhsT=xcodes[:, xs].bitcast(FP8X4),
+                lhsT_scale=xscl[:, xs],
+                rhs=wcodes[:, w0:w0 + 512].bitcast(FP8X4),
+                rhs_scale=wscl[:, w0:w0 + 512],
+                start=start,
+                stop=stop,
+            )
+
+        def mm(t, i, three):
+            tb = accp.tile([P, 512], F32, name="tb")
+            ta = accp.tile([P, 512], F32, name="ta")
+            for x, bank in ((0, tb), (1, ta)):
+                mx(bank, t, i, 0, x, True, False)
+                mx(bank, t, i, 1, x, False, True)
+            if not three:
+                return tb, ta, None
+            uu = uup.tile([P, 512], F32, name="uu")
+            mx(uu, t, i, 0, 0, True, False)
+            mx(uu, t, i, 0, 1, False, False)
+            mx(uu, t, i, 1, 0, False, False)
+            mx(uu, t, i, 1, 1, False, True)
+            return tb, ta, uu
+
+        def by_heads(ap):
+            return ap.rearrange("p (h j) -> p h j", j=64)
+
+        def mult(out, bank, table):
+            nc.vector.tensor_tensor(
+                out=by_heads(out), in0=by_heads(bank[:]), in1=table.to_broadcast([P, 8, 64]), op=ALU.mult
+            )
+
+        def first_products(i, banks):
+            tb, ta, uu = banks
+            kk = p3.tile([P, 2, 512], F32, name="kk")
+            if uu is None:
+                k2 = p3.tile([P, 2, 512], F32, name="k2")
+                mult(kk[:, 0, :], tb, stab[:, i, 0])
+                mult(k2[:, 1, :], tb, ctab[:, i, 0])
+                mult(kk[:, 1, :], ta, stab[:, i, 1])
+                return kk, k2
+            mult(kk[:, 0, :], tb, ttab[:, i, 0])
+            mult(kk[:, 1, :], ta, ttab[:, i, 1])
+            return kk, None
+
+        def last_product(i, banks, k2):
+            tb, ta, uu = banks
+            if uu is None:
+                mult(k2[:, 0, :], ta, ctab[:, i, 0])
+                return k2[:]
+            k1 = p3.tile([P, 1, 512], F32, name="k1")
+            mult(k1[:, 0, :], uu, ctab[:, i, 0])
+            return k1[:].to_broadcast([P, 2, 512])
+
+        outv = [o[0].rearrange("h (p i) d -> p h i d", i=8) for o in (out_0, out_1)]
+
+        def add_v(kk, other, hs):
+            sm = p3.tile([P, 2, 512], F32, name="sm")
+            for h0, h1 in hs:
+                cols = slice(64 * h0, 64 * h1)
+                nc.vector.tensor_tensor(out=sm[:, :, cols], in0=kk[:, :, cols], in1=other[:, :, cols], op=ALU.add)
+            return sm
+
+        def add_g(kk, other):
+            sm = p3.tile([P, 2, 512], F32, name="sm")
+            for x in range(2):
+                nc.gpsimd.tensor_tensor(out=sm[:, x, :], in0=kk[:, x, :], in1=other[:, x, :], op=ALU.add)
+            return sm
+
+        def relu(sm, dst, h0, h1):
+            nc.scalar.activation(
+                out=dst[:, h0:h1, :].rearrange("p h (j e) -> p h j e", e=2),
+                in_=sm[:, :, 64 * h0:64 * h1].rearrange("p e (h j) -> p h j e", j=64),
+                func=ACT.Relu,
+            )
+
+        with tc.psum_pool(name="tp1", bufs=4) as tp1:
+            turn_w(tp1, 0, 0)
+            turn_w(tp1, 0, 1)
+            for q in range(4):
+                xws = [widen(2 * q), widen(2 * q + 1)]
+                turn_x(tp1, 2 * q, xws[0])
+                turn_x(tp1, 2 * q + 1, xws[1])
+                if q < 3:
+                    turn_w(tp1, 0, 2 * q + 2)
+                    turn_w(tp1, 0, 2 * q + 3)
+        quant_x(0)
+        quant_w(0, 0)
+        quant_w(0, 1)
+        quant_x(1)
+        uup = ctx.enter_context(tc.psum_pool(name="uup", bufs=2))
+        tp2 = ctx.enter_context(tc.psum_pool(name="tp2", bufs=2))
+        for h in range(8):
+            turn_w(tp2, 1, h)
+
+        whole = ((0, 8),)
+        halves = ((0, 4), (4, 8))
+        for pair in range(8):
+            t, i = pair // 4, 2 * (pair % 4)
+            last = pair == 7
+            ost = p2.tile([P, 8, 2, P], F32, name="ost")
+            banks_a = mm(t, i, 2 * pair >= PLAIN_UNITS)
+            kka, k2a = first_products(i, banks_a)
+            oa = last_product(i, banks_a, k2a)
+            banks_b = mm(t, i + 1, 2 * pair + 1 >= PLAIN_UNITS)
+            kkb, k2b = first_products(i + 1, banks_b)
+            sma = add_v(kka, oa, whole)
+            relu(sma, ost[:, :, 0, :], 0, 8)
+            if pair in (1, 2):
+                quant_w(1, pair - 1)
+            ob = last_product(i + 1, banks_b, k2b)
+            if not last:
+                smb = add_g(kkb, ob)
+                relu(smb, ost[:, :, 1, :], 0, 8)
+                nc.sync.dma_start(out=outv[t][:, :, i:i + 2, :], in_=ost[:])
+            else:
+                nc.sync.dma_start(out=outv[t][:, :, i, :], in_=ost[:, :, 0, :])
+                smb = add_v(kkb, ob, halves)
+                for h0, h1 in halves:
+                    relu(smb, ost[:, :, 1, :], h0, h1)
+                    nc.sync.dma_start(out=outv[t][:, h0:h1, i + 1, :], in_=ost[:, h0:h1, 1, :])

@@ -273,11 +273,11 @@ def tile_linearattention_pa_kernel(tc, x_bytes, x_scale, wq, wk, out_0, out_1):
             oa = last_product(i, banks_a, k2a)
             banks_b = mm(t, i + 1, 2 * pair + 1 >= PLAIN_UNITS)
             kkb, k2b = first_products(i + 1, banks_b)
+            ob = last_product(i + 1, banks_b, k2b)
             sma = add_v(kka, oa, whole)
             relu(sma, ost[:, :, 0, :], 0, 8)
             if pair in (1, 2):
                 quant_w(1, pair - 1)
-            ob = last_product(i + 1, banks_b, k2b)
             if not last:
                 smb = add_g(kkb, ob)
                 relu(smb, ost[:, :, 1, :], 0, 8)

@@ -18,13 +18,13 @@ ACT = mybir.ActivationFunctionType
 
 P = 128
 TWO_PI = 2.0 * math.pi
-PLAIN_UNITS = 3
+PLAIN_UNITS = 2
 
 
 def tile_linearattention_pa_kernel(tc, x_bytes, x_scale, wq, wk, out_0, out_1):
     nc = tc.nc
     with ExitStack() as ctx:
-        ctx.enter_context(tc.manual_schedule(engines={mybir.EngineType.DVE}))
+        ctx.enter_context(tc.manual_schedule(engines={mybir.EngineType.DVE, mybir.EngineType.PE}))
         const = ctx.enter_context(tc.tile_pool(name="const", bufs=1))
         p2 = ctx.enter_context(tc.tile_pool(name="p2", bufs=2))
         p3 = ctx.enter_context(tc.tile_pool(name="p3", bufs=3))
@@ -253,14 +253,16 @@ def tile_linearattention_pa_kernel(tc, x_bytes, x_scale, wq, wk, out_0, out_1):
                 if q < 3:
                     turn_w(tp1, 0, 2 * q + 2)
                     turn_w(tp1, 0, 2 * q + 3)
-        quant_x(0)
-        quant_w(0, 0)
-        quant_w(0, 1)
-        quant_x(1)
+            quant_x(0)
+            quant_w(0, 0)
+            quant_w(0, 1)
+            quant_x(1)
+            for h in range(4):
+                turn_w(tp1, 1, h)
+            first_banks = [mm(0, 0, False), mm(0, 1, False)]
+            for h in range(4, 8):
+                turn_w(tp1, 1, h)
         uup = ctx.enter_context(tc.psum_pool(name="uup", bufs=2))
-        tp2 = ctx.enter_context(tc.psum_pool(name="tp2", bufs=2))
-        for h in range(8):
-            turn_w(tp2, 1, h)
 
         whole = ((0, 8),)
         halves = ((0, 4), (4, 8))
@@ -268,10 +270,10 @@ def tile_linearattention_pa_kernel(tc, x_bytes, x_scale, wq, wk, out_0, out_1):
             t, i = pair // 4, 2 * (pair % 4)
             last = pair == 7
             ost = p2.tile([P, 8, 2, P], F32, name="ost")
-            banks_a = mm(t, i, 2 * pair >= PLAIN_UNITS)
+            banks_a = first_banks[0] if pair == 0 else mm(t, i, 2 * pair >= PLAIN_UNITS)
             kka, k2a = first_products(i, banks_a)
             oa = last_product(i, banks_a, k2a)
-            banks_b = mm(t, i + 1, 2 * pair + 1 >= PLAIN_UNITS)
+            banks_b = first_banks[1] if pair == 0 else mm(t, i + 1, 2 * pair + 1 >= PLAIN_UNITS)
             kkb, k2b = first_products(i + 1, banks_b)
             ob = last_product(i + 1, banks_b, k2b)
             sma = add_v(kka, oa, whole)

@@ -243,6 +243,13 @@ def tile_linearattention_pa_kernel(tc, x_bytes, x_scale, wq, wk, out_0, out_1):
                 func=ACT.Relu,
             )
 
+        def relu_v(sm, dst, h0, h1):
+            nc.vector.tensor_scalar_max(
+                out=dst[:, h0:h1, :].rearrange("p h (j e) -> p h j e", e=2),
+                in0=sm[:, :, 64 * h0:64 * h1].rearrange("p e (h j) -> p h j e", j=64),
+                scalar1=0.0,
+            )
+
         with tc.psum_pool(name="tp1", bufs=4) as tp1:
             turn_w(tp1, 0, 0)
             turn_w(tp1, 0, 1)
@@ -266,27 +273,43 @@ def tile_linearattention_pa_kernel(tc, x_bytes, x_scale, wq, wk, out_0, out_1):
 
         whole = ((0, 8),)
         halves = ((0, 4), (4, 8))
-        for pair in range(8):
-            t, i = pair // 4, 2 * (pair % 4)
-            last = pair == 7
-            ost = p2.tile([P, 8, 2, P], F32, name="ost")
-            banks_a = first_banks[0] if pair == 0 else mm(t, i, 2 * pair >= PLAIN_UNITS)
-            kka, k2a = first_products(i, banks_a)
-            oa = last_product(i, banks_a, k2a)
-            banks_b = first_banks[1] if pair == 0 else mm(t, i + 1, 2 * pair + 1 >= PLAIN_UNITS)
-            kkb, k2b = first_products(i + 1, banks_b)
-            ob = last_product(i + 1, banks_b, k2b)
-            sma = add_v(kka, oa, whole)
-            relu(sma, ost[:, :, 0, :], 0, 8)
-            if pair in (1, 2):
-                quant_w(1, pair - 1)
-            if not last:
-                smb = add_g(kkb, ob)
-                relu(smb, ost[:, :, 1, :], 0, 8)
-                nc.sync.dma_start(out=outv[t][:, :, i:i + 2, :], in_=ost[:])
-            else:
-                nc.sync.dma_start(out=outv[t][:, :, i, :], in_=ost[:, :, 0, :])
-                smb = add_v(kkb, ob, halves)
+        osts = {}
+
+        def finish(n, sm):
+            t, i = n // 8, n % 8
+            relu(sm, osts[n // 2][:, :, n % 2, :], 0, 8)
+            done.add(n)
+            if n >= 14:
+                nc.sync.dma_start(out=outv[t][:, :, i, :], in_=osts[n // 2][:, :, n % 2, :])
+            elif (n ^ 1) in done:
+                i0 = i - n % 2
+                nc.sync.dma_start(out=outv[t][:, :, i0:i0 + 2, :], in_=osts[n // 2][:])
+
+        done = set()
+        waiting = []
+        for n in range(16):
+            t, i = n // 8, n % 8
+            if n % 2 == 0:
+                ost = p2.tile([P, 8, 2, P], F32, name="ost")
+                osts[n // 2] = ost
+            banks = first_banks[n] if n < 2 else mm(t, i, n >= PLAIN_UNITS)
+            kk, k2 = first_products(i, banks)
+            if n == 15:
+                m, kkm, om = waiting.pop()
+                finish(m, add_v(kkm, om, whole))
+            other = last_product(i, banks, k2)
+            if waiting:
+                m, kkm, om = waiting.pop()
+                finish(m, add_v(kkm, om, whole))
+                if m == 3:
+                    quant_w(1, 0)
+                    quant_w(1, 1)
+            if n == 15:
+                sm = add_v(kk, other, halves)
                 for h0, h1 in halves:
-                    relu(smb, ost[:, :, 1, :], h0, h1)
-                    nc.sync.dma_start(out=outv[t][:, h0:h1, i + 1, :], in_=ost[:, h0:h1, 1, :])
+                    (relu if h0 == 0 else relu_v)(sm, osts[7][:, :, 1, :], h0, h1)
+                    nc.sync.dma_start(out=outv[t][:, h0:h1, i, :], in_=osts[7][:, h0:h1, 1, :])
+            elif n % 3 == 0 or n == 14:
+                waiting.append((n, kk, other))
+            else:
+                finish(n, add_g(kk, other))

@@ -27,7 +27,7 @@ def tile_linearattention_pa_kernel(tc, x_bytes, x_scale, wq, wk, out_0, out_1):
         ctx.enter_context(tc.manual_schedule(engines={mybir.EngineType.DVE, mybir.EngineType.PE}))
         const = ctx.enter_context(tc.tile_pool(name="const", bufs=1))
         p2 = ctx.enter_context(tc.tile_pool(name="p2", bufs=2))
-        p3 = ctx.enter_context(tc.tile_pool(name="p3", bufs=3))
+        p3 = ctx.enter_context(tc.tile_pool(name="p3", bufs=5))
         p8 = ctx.enter_context(tc.tile_pool(name="p8", bufs=8))
         accp = ctx.enter_context(tc.psum_pool(name="accp", bufs=2))
 
@@ -59,10 +59,13 @@ def tile_linearattention_pa_kernel(tc, x_bytes, x_scale, wq, wk, out_0, out_1):
         for rt in range(6, 16):
             load_w(rt)
 
-        posi = const.tile([P, 8], I32, name="posi")
-        nc.gpsimd.iota(posi[:], pattern=[[1, 8]], base=0, channel_multiplier=8)
+        posf = const.tile([P, 8, 1], F32, name="posf")
+        nc.gpsimd.iota(
+            posf[:].rearrange("p i o -> p (i o)"), pattern=[[1, 8]], base=0, channel_multiplier=8,
+            allow_small_or_imprecise_dtypes=True,
+        )
         one = const.tile([P, 1], F32, name="one")
-        nc.vector.memset(one[:], 1.0)
+        nc.gpsimd.memset(one[:], 1.0)
         warm = const.tile([P, 1], F32, name="warm")
         nc.scalar.activation(out=warm[:], in_=one[:], func=ACT.Sin)
 
@@ -72,29 +75,49 @@ def tile_linearattention_pa_kernel(tc, x_bytes, x_scale, wq, wk, out_0, out_1):
         nc.scalar.copy(out=perm[:, 0:64], in_=ident[:, 1:128:2])
         nc.scalar.copy(out=perm[:, 64:128], in_=ident[:, 0:128:2])
 
-
-        th = const.tile([P, 1, 64], F32, name="th")
-        thf = th[:].rearrange("p o j -> p (o j)")
-        nc.vector.memset(thf, 1.0)
-        nc.vector.tensor_scalar_mul(out=thf, in0=thf, scalar1=1.0 / TWO_PI)
-        for b in range(6):
-            half = thf.rearrange("p (a two l) -> p a two l", two=2, l=1 << b)[:, :, 1, :]
-            nc.vector.tensor_scalar_mul(out=half, in0=half, scalar1=10000.0 ** (-(1 << b) / 64.0))
-
-        posf = const.tile([P, 8, 1], F32, name="posf")
-        nc.vector.tensor_copy(out=posf[:].rearrange("p i o -> p (i o)"), in_=posi[:])
-        tau = const.tile([P, 8, 64], F32, name="tau")
+        abc = const.tile([P, 12], F32, name="abc")
+        nc.vector.memset(abc[:], 1.0)
+        for b in range(2):
+            for f in range(3):
+                half = abc[:, 4 * f:4 * f + 4].rearrange("p (a two l) -> p a two l", two=2, l=1 << b)[:, :, 1, :]
+                nc.vector.tensor_scalar_mul(out=half, in0=half, scalar1=10000.0 ** (-((16, 4, 1)[f] << b) / 64.0))
+        bc = const.tile([P, 4, 4], F32, name="bc")
         nc.vector.tensor_tensor(
-            out=tau[:], in0=th[:].to_broadcast([P, 8, 64]), in1=posf[:].to_broadcast([P, 8, 64]), op=ALU.mult
+            out=bc[:], in0=abc[:, 4:8].unsqueeze(2).to_broadcast([P, 4, 4]),
+            in1=abc[:, 8:12].unsqueeze(1).to_broadcast([P, 4, 4]), op=ALU.mult,
         )
-        ki = const.tile([P, 8, 64], I32, name="ki")
-        nc.vector.tensor_copy(out=ki[:], in_=tau[:])
-        fr = const.tile([P, 8, 64], F32, name="fr")
-        nc.vector.tensor_tensor(out=fr[:], in0=tau[:], in1=ki[:], op=ALU.subtract)
+        pa = const.tile([P, 8, 4], F32, name="pa")
+        nc.vector.scalar_tensor_tensor(
+            out=pa[:], in0=posf[:].to_broadcast([P, 8, 4]), scalar=1.0 / TWO_PI,
+            in1=abc[:, 0:4].unsqueeze(1).to_broadcast([P, 8, 4]), op0=ALU.mult, op1=ALU.mult,
+        )
+        tau = const.tile([P, 32, 16], F32, name="tau")
+        ki = const.tile([P, 512], I32, name="ki")
+        fr = const.tile([P, 512], F32, name="fr")
         ng = const.tile([P, 8, 64], F32, name="ng")
-        nc.vector.scalar_tensor_tensor(out=ng[:], in0=fr[:], scalar=0.5, in1=fr[:], op0=ALU.is_gt, op1=ALU.subtract)
         ab = const.tile([P, 8, 64], F32, name="ab")
-        nc.vector.scalar_tensor_tensor(out=ab[:], in0=ng[:], scalar=-1.0, in1=ng[:], op0=ALU.mult, op1=ALU.max)
+        tauf = tau[:].rearrange("p r q -> p (r q)")
+        ngf = ng[:].rearrange("p i j -> p (i j)")
+        abf = ab[:].rearrange("p i j -> p (i j)")
+        table_halves = (slice(0, 256), slice(256, 512))
+        for z in range(2):
+            nc.vector.tensor_tensor(
+                out=tau[:, 16 * z:16 * z + 16, :],
+                in0=pa[:].rearrange("p i a -> p (i a)")[:, 16 * z:16 * z + 16].unsqueeze(2).to_broadcast([P, 16, 16]),
+                in1=bc[:].rearrange("p b c -> p (b c)").unsqueeze(1).to_broadcast([P, 16, 16]), op=ALU.mult,
+            )
+        for cols in table_halves:
+            nc.vector.tensor_copy(out=ki[:, cols], in_=tauf[:, cols])
+        for cols in table_halves:
+            nc.vector.tensor_tensor(out=fr[:, cols], in0=tauf[:, cols], in1=ki[:, cols], op=ALU.subtract)
+        for cols in table_halves:
+            nc.vector.scalar_tensor_tensor(
+                out=ngf[:, cols], in0=fr[:, cols], scalar=0.5, in1=fr[:, cols], op0=ALU.is_gt, op1=ALU.subtract
+            )
+        for cols in table_halves:
+            nc.vector.scalar_tensor_tensor(
+                out=abf[:, cols], in0=ngf[:, cols], scalar=-1.0, in1=ngf[:, cols], op0=ALU.mult, op1=ALU.max
+            )
 
         ctab = const.tile([P, 8, 1, 1, 64], F32, name="ctab")
         nc.scalar.activation(
@@ -203,7 +226,7 @@ def tile_linearattention_pa_kernel(tc, x_bytes, x_scale, wq, wk, out_0, out_1):
             tb, ta, uu = banks
             kk = p3.tile([P, 2, 512], F32, name="kk")
             if uu is None:
-                k2 = p3.tile([P, 2, 512], F32, name="k2")
+                k2 = p2.tile([P, 2, 512], F32, name="k2")
                 mult(kk[:, 0, :], tb, stab[:, i, 0])
                 mult(k2[:, 1, :], tb, ctab[:, i, 0])
                 mult(kk[:, 1, :], ta, stab[:, i, 1])

@@ -118,22 +118,31 @@ def tile_linearattention_pa_kernel(tc, x_bytes, x_scale, wq, wk, out_0, out_1):
             nc.vector.scalar_tensor_tensor(
                 out=abf[:, cols], in0=ngf[:, cols], scalar=-1.0, in1=ngf[:, cols], op0=ALU.mult, op1=ALU.max
             )
+        for cols in table_halves:
+            nc.vector.scalar_tensor_tensor(
+                out=tauf[:, cols], in0=ngf[:, cols], scalar=-0.375, in1=ngf[:, cols], op0=ALU.is_lt, op1=ALU.add
+            )
+        for cols in table_halves:
+            nc.vector.scalar_tensor_tensor(
+                out=fr[:, cols], in0=ngf[:, cols], scalar=0.375, in1=ngf[:, cols], op0=ALU.is_gt, op1=ALU.subtract
+            )
 
         ctab = const.tile([P, 8, 1, 1, 64], F32, name="ctab")
         nc.scalar.activation(
             out=ctab[:].rearrange("p i a b j -> p i (a b j)"), in_=ab[:], func=ACT.Sin, bias=math.pi / 2.0, scale=-TWO_PI
         )
-        stab = const.tile([P, 8, 2, 1, 64], F32, name="stab")
-        sview = stab[:].rearrange("p i x o j -> p i x (o j)")
-        nc.scalar.activation(out=sview[:, :, 0, :], in_=ng[:], func=ACT.Sin, scale=TWO_PI)
-        nc.scalar.activation(out=sview[:, :, 1, :], in_=ng[:], func=ACT.Sin, scale=-TWO_PI)
         ttab = const.tile([P, 8, 2, 1, 64], F32, name="ttab")
-        nc.gpsimd.tensor_tensor(
-            out=ttab[:].rearrange("p i x o j -> p i x (o j)"),
-            in0=sview,
-            in1=ctab[:].rearrange("p i a b j -> p i a (b j)").to_broadcast([P, 8, 2, 64]),
-            op=ALU.subtract,
+        tview = ttab[:].rearrange("p i x o j -> p i x (o j)")
+        nc.scalar.activation(
+            out=tview[:, :, 0, :], in_=tauf.rearrange("p (i j) -> p i j", j=64), func=ACT.Sin, bias=-math.pi / 4.0, scale=TWO_PI
         )
+        nc.scalar.activation(
+            out=tview[:, :, 1, :], in_=fr[:].rearrange("p (i j) -> p i j", j=64), func=ACT.Sin, bias=-math.pi / 4.0, scale=TWO_PI
+        )
+        stab = const.tile([P, PLAIN_UNITS, 2, 1, 64], F32, name="stab")
+        sview = stab[:].rearrange("p i x o j -> p i x (o j)")
+        nc.scalar.activation(out=sview[:, :, 0, :], in_=ng[:, 0:PLAIN_UNITS, :], func=ACT.Sin, scale=TWO_PI)
+        nc.scalar.activation(out=sview[:, :, 1, :], in_=ng[:, 0:PLAIN_UNITS, :], func=ACT.Sin, scale=-TWO_PI)
 
         xcodes = const.tile([P, 2048], U32, name="xcodes", align_bytes=64)
         xscl = const.tile([P, 2048], U8, name="xscl", align_bytes=64)
@@ -222,6 +231,12 @@ def tile_linearattention_pa_kernel(tc, x_bytes, x_scale, wq, wk, out_0, out_1):
                 out=by_heads(out), in0=by_heads(bank[:]), in1=table.to_broadcast([P, 8, 64]), op=ALU.mult
             )
 
+        def mult_root2(out, bank, table):
+            nc.vector.scalar_tensor_tensor(
+                out=by_heads(out), in0=by_heads(bank[:]), scalar=math.sqrt(2.0), in1=table.to_broadcast([P, 8, 64]),
+                op0=ALU.mult, op1=ALU.mult,
+            )
+
         def first_products(i, banks):
             tb, ta, uu = banks
             kk = p3.tile([P, 2, 512], F32, name="kk")
@@ -231,8 +246,8 @@ def tile_linearattention_pa_kernel(tc, x_bytes, x_scale, wq, wk, out_0, out_1):
                 mult(k2[:, 1, :], tb, ctab[:, i, 0])
                 mult(kk[:, 1, :], ta, stab[:, i, 1])
                 return kk, k2
-            mult(kk[:, 0, :], tb, ttab[:, i, 0])
-            mult(kk[:, 1, :], ta, ttab[:, i, 1])
+            mult_root2(kk[:, 0, :], tb, ttab[:, i, 0])
+            mult_root2(kk[:, 1, :], ta, ttab[:, i, 1])
             return kk, None
 
         def last_product(i, banks, k2):

@@ -317,7 +317,7 @@ def tile_linearattention_pa_kernel(tc, x_bytes, x_scale, wq, wk, out_0, out_1):
             t, i = n // 8, n % 8
             relu(sm, osts[n // 2][:, :, n % 2, :], 0, 8)
             done.add(n)
-            if n >= 14:
+            if n >= 12:
                 nc.sync.dma_start(out=outv[t][:, :, i, :], in_=osts[n // 2][:, :, n % 2, :])
             elif (n ^ 1) in done:
                 i0 = i - n % 2

@@ -51,7 +51,7 @@ def tile_linearattention_pa_kernel(tc, x_bytes, x_scale, wq, wk, out_0, out_1):
             nc.sync.dma_start(out=wraw[rt][:], in_=src[r0:r0 + 128, :])
 
         load_x(0)
-        nc.sync.dma_start(out=xsc[:], in_=x_scale[0].rearrange("o k -> (o k)").partition_broadcast(P))
+        nc.scalar.dma_start(out=xsc[:], in_=x_scale[0].rearrange("o k -> (o k)").partition_broadcast(P))
         for q in range(1, 4):
             load_w(2 * q - 2)
             load_w(2 * q - 1)

@@ -36,6 +36,7 @@ def tile_linearattention_pa_kernel(tc, x_bytes, x_scale, wq, wk, out_0, out_1):
         for q in range(4):
             xbq = const.tile([P, 2048], U8, name="xbytes%d" % q)
             xby.append(xbq)
+        sct = const.tile([P, 2, 4], F32, name="sct")
         xsc = const.tile([P, 1024], F32, name="xsc")
         wraw = []
         for rt in range(16):
@@ -51,7 +52,7 @@ def tile_linearattention_pa_kernel(tc, x_bytes, x_scale, wq, wk, out_0, out_1):
             nc.sync.dma_start(out=wraw[rt][:], in_=src[r0:r0 + 128, :])
 
         load_x(0)
-        nc.scalar.dma_start(out=xsc[:], in_=x_scale[0].rearrange("o k -> (o k)").partition_broadcast(P))
+        nc.scalar.dma_start(out=sct[:], in_=x_scale[0].rearrange("o (g p t) -> p (o g) t", g=2, t=4))
         for q in range(1, 4):
             load_w(2 * q - 2)
             load_w(2 * q - 1)
@@ -148,6 +149,15 @@ def tile_linearattention_pa_kernel(tc, x_bytes, x_scale, wq, wk, out_0, out_1):
         xscl = const.tile([P, 2048], U8, name="xscl", align_bytes=64)
         wcodes = const.tile([P, 4096], U32, name="wcodes", align_bytes=64)
         wscl = const.tile([P, 4096], U8, name="wscl", align_bytes=64)
+
+        def spread_scales(pool):
+            for g in range(2):
+                bank = pool.tile([P, 4, P], F32, name="tp")
+                for t in range(4):
+                    nc.tensor.transpose(bank[:, t, :], sct[:, g, t:t + 1].to_broadcast([P, P]), ident[:])
+                nc.scalar.copy(
+                    out=xsc[:, 512 * g:512 * (g + 1)].rearrange("p (w t) -> p w t", t=4), in_=bank[:].rearrange("p t w -> p w t")
+                )
 
         def widen(i):
             xw = p8.tile([P, 1024], BF16, name="xw")
@@ -289,6 +299,7 @@ def tile_linearattention_pa_kernel(tc, x_bytes, x_scale, wq, wk, out_0, out_1):
             )
 
         with tc.psum_pool(name="tp1", bufs=4) as tp1:
+            spread_scales(tp1)
             turn_w(tp1, 0, 0)
             turn_w(tp1, 0, 1)
             for q in range(4):

@@ -18,18 +18,20 @@ ACT = mybir.ActivationFunctionType
 
 P = 128
 TWO_PI = 2.0 * math.pi
-PLAIN_UNITS = 2
+VECTOR_ADDS = (4, 5, 8, 11, 14)
+PLAIN = (0, 2, 3)
+PLAIN_UNITS = 4
 
 
 def tile_linearattention_pa_kernel(tc, x_bytes, x_scale, wq, wk, out_0, out_1):
     nc = tc.nc
     with ExitStack() as ctx:
-        ctx.enter_context(tc.manual_schedule(engines={mybir.EngineType.DVE, mybir.EngineType.PE}))
+        ctx.enter_context(tc.manual_schedule(engines={mybir.EngineType.DVE, mybir.EngineType.PE, mybir.EngineType.Activation}))
         const = ctx.enter_context(tc.tile_pool(name="const", bufs=1))
         p2 = ctx.enter_context(tc.tile_pool(name="p2", bufs=2))
         p3 = ctx.enter_context(tc.tile_pool(name="p3", bufs=5))
         p8 = ctx.enter_context(tc.tile_pool(name="p8", bufs=8))
-        accp = ctx.enter_context(tc.psum_pool(name="accp", bufs=2))
+        psum = ctx.enter_context(tc.psum_pool(name="psum", bufs=8))
 
         xv = x_bytes[0].rearrange("(p i) k -> p (i k)", i=8)
         xby = []
@@ -53,11 +55,14 @@ def tile_linearattention_pa_kernel(tc, x_bytes, x_scale, wq, wk, out_0, out_1):
 
         load_x(0)
         nc.scalar.dma_start(out=sct[:], in_=x_scale[0].rearrange("o (g p t) -> p (o g) t", g=2, t=4))
-        for q in range(1, 4):
-            load_w(2 * q - 2)
-            load_w(2 * q - 1)
-            load_x(q)
-        for rt in range(6, 16):
+        load_w(0)
+        load_w(1)
+        load_x(1)
+        for rt in range(2, 8):
+            load_w(rt)
+        load_x(2)
+        load_x(3)
+        for rt in range(8, 16):
             load_w(rt)
 
         posf = const.tile([P, 8, 1], F32, name="posf")
@@ -129,35 +134,52 @@ def tile_linearattention_pa_kernel(tc, x_bytes, x_scale, wq, wk, out_0, out_1):
             )
 
         ctab = const.tile([P, 8, 1, 1, 64], F32, name="ctab")
-        nc.scalar.activation(
-            out=ctab[:].rearrange("p i a b j -> p i (a b j)"), in_=ab[:], func=ACT.Sin, bias=math.pi / 2.0, scale=-TWO_PI
-        )
         ttab = const.tile([P, 8, 2, 1, 64], F32, name="ttab")
         tview = ttab[:].rearrange("p i x o j -> p i x (o j)")
-        nc.scalar.activation(
-            out=tview[:, :, 0, :], in_=tauf.rearrange("p (i j) -> p i j", j=64), func=ACT.Sin, bias=-math.pi / 4.0, scale=TWO_PI
-        )
-        nc.scalar.activation(
-            out=tview[:, :, 1, :], in_=fr[:].rearrange("p (i j) -> p i j", j=64), func=ACT.Sin, bias=-math.pi / 4.0, scale=TWO_PI
-        )
         stab = const.tile([P, PLAIN_UNITS, 2, 1, 64], F32, name="stab")
         sview = stab[:].rearrange("p i x o j -> p i x (o j)")
-        nc.scalar.activation(out=sview[:, :, 0, :], in_=ng[:, 0:PLAIN_UNITS, :], func=ACT.Sin, scale=TWO_PI)
-        nc.scalar.activation(out=sview[:, :, 1, :], in_=ng[:, 0:PLAIN_UNITS, :], func=ACT.Sin, scale=-TWO_PI)
+
+        def rope_tables():
+            nc.scalar.activation(
+                out=ctab[:].rearrange("p i a b j -> p i (a b j)"), in_=ab[:], func=ACT.Sin, bias=math.pi / 2.0, scale=-TWO_PI
+            )
+            nc.scalar.activation(out=sview[:, :, 0, :], in_=ng[:, 0:PLAIN_UNITS, :], func=ACT.Sin, scale=TWO_PI)
+            nc.scalar.activation(out=sview[:, :, 1, :], in_=ng[:, 0:PLAIN_UNITS, :], func=ACT.Sin, scale=-TWO_PI)
+            nc.scalar.activation(
+                out=tview[:, :, 0, :], in_=tauf.rearrange("p (i j) -> p i j", j=64), func=ACT.Sin, bias=-math.pi / 4.0, scale=TWO_PI
+            )
+            nc.scalar.activation(
+                out=tview[:, :, 1, :], in_=fr[:].rearrange("p (i j) -> p i j", j=64), func=ACT.Sin, bias=-math.pi / 4.0, scale=TWO_PI
+            )
 
         xcodes = const.tile([P, 2048], U32, name="xcodes", align_bytes=64)
         xscl = const.tile([P, 2048], U8, name="xscl", align_bytes=64)
         wcodes = const.tile([P, 4096], U32, name="wcodes", align_bytes=64)
         wscl = const.tile([P, 4096], U8, name="wscl", align_bytes=64)
 
-        def spread_scales(pool):
+        def new_bank():
+            bank = psum.tile([P, 512], F32, name="bank")
+            return bank
+
+        def turn(words, eye, u_major):
+            bank = new_bank()
             for g in range(2):
-                bank = pool.tile([P, 4, P], F32, name="tp")
+                for u in range(2):
+                    slot = 2 * u + g if u_major else 2 * g + u
+                    nc.tensor.transpose(bank[:, P * slot:P * (slot + 1)], words[:, 256 * g + u:256 * (g + 1):2], eye[:])
+            return bank
+
+        def spread_scales():
+            for g in range(2):
+                bank = new_bank()
                 for t in range(4):
-                    nc.tensor.transpose(bank[:, t, :], sct[:, g, t:t + 1].to_broadcast([P, P]), ident[:])
+                    nc.tensor.transpose(bank[:, P * t:P * (t + 1)], sct[:, g, t:t + 1].to_broadcast([P, P]), ident[:])
                 nc.scalar.copy(
-                    out=xsc[:, 512 * g:512 * (g + 1)].rearrange("p (w t) -> p w t", t=4), in_=bank[:].rearrange("p t w -> p w t")
+                    out=xsc[:, 512 * g:512 * (g + 1)].rearrange("p (w t) -> p w t", t=4), in_=bank[:].rearrange("p (t w) -> p w t", t=4)
                 )
+
+        xws = {}
+        xgs = {}
 
         def widen(i):
             xw = p8.tile([P, 1024], BF16, name="xw")
@@ -165,25 +187,39 @@ def tile_linearattention_pa_kernel(tc, x_bytes, x_scale, wq, wk, out_0, out_1):
             nc.vector.tensor_tensor(
                 out=xw[:], in0=xby[i // 2][:, lo:lo + 1024].bitcast(FP8), in1=xsc[:], op=ALU.mult
             )
-            return xw
+            xws[i] = xw
 
-        def turn(pool, words, eye, u_major):
-            bank = pool.tile([P, 4, P], F32, name="tp")
+        xbanks = {}
+
+        def cast_x(i):
+            xw = p8.tile([P, 1024], BF16, name="xw")
+            lo = 1024 * (i % 2)
+            nc.scalar.copy(out=xw[:], in_=xby[i // 2][:, lo:lo + 1024].bitcast(FP8))
+            xws[i] = xw
+
+        def turn_unscaled(i):
+            xbanks[i] = turn(xws[i][:].bitcast(F32), ident, False)
+
+        def scale_x(i):
+            if i % 4 == 0:
+                xg = p2.tile([P, 4096], BF16, name="xg", align_bytes=64)
+                xgs[i // 4] = xg
             for g in range(2):
-                for u in range(2):
-                    slot = 2 * u + g if u_major else 2 * g + u
-                    nc.tensor.transpose(bank[:, slot, :], words[:, 256 * g + u:256 * (g + 1):2], eye[:])
-            return bank
+                lo = 1024 * (i % 4) + 512 * g
+                nc.vector.tensor_tensor(
+                    out=xgs[i // 4][:, lo:lo + 512].rearrange("p (r u e) -> p r u e", u=2, e=2),
+                    in0=xbanks[i][:, 256 * g:256 * (g + 1)].bitcast(BF16).rearrange("p (u r e) -> p r u e", u=2, e=2),
+                    in1=sct[:, g, :].rearrange("p (o u e) -> p o u e", o=1, e=2).to_broadcast([P, P, 2, 2]),
+                    op=ALU.mult,
+                )
 
-        xgs = {}
-
-        def turn_x(pool, i, xw):
+        def turn_x(i):
             if i % 4 == 0:
                 xg = p2.tile([P, 4096], BF16, name="xg", align_bytes=64)
                 xgs[i // 4] = xg
             xgw = xgs[i // 4][:].bitcast(F32).rearrange("p (i g r u) -> p i g r u", i=4, g=2, u=2)
-            bank = turn(pool, xw[:].bitcast(F32), ident, False)
-            nc.scalar.copy(out=xgw[:, i % 4], in_=bank[:].rearrange("p (g u) r -> p g r u", u=2))
+            bank = turn(xws[i][:].bitcast(F32), ident, False)
+            nc.scalar.copy(out=xgw[:, i % 4], in_=bank[:].rearrange("p (g u r) -> p g r u", g=2, u=2))
 
         def quant_x(q):
             cols = slice(1024 * q, 1024 * (q + 1))
@@ -191,13 +227,13 @@ def tile_linearattention_pa_kernel(tc, x_bytes, x_scale, wq, wk, out_0, out_1):
 
         wgs = {}
 
-        def turn_w(pool, t, h):
+        def turn_w(t, h):
             if h == 0:
                 wg = p2.tile([P, 8192], BF16, name="wg", align_bytes=64)
                 wgs[t] = wg
             wgw = wgs[t][:].bitcast(F32).rearrange("p (gx h j u) -> p gx h j u", gx=4, h=8, u=2)
-            bank = turn(pool, wraw[8 * t + h][:].bitcast(F32), perm, True)
-            nc.scalar.copy(out=wgw[:, :, h], in_=bank[:].rearrange("p (u g) (x j) -> p u (g x) j", u=2, x=2).rearrange("p u gx j -> p gx j u"))
+            bank = turn(wraw[8 * t + h][:].bitcast(F32), perm, True)
+            nc.scalar.copy(out=wgw[:, :, h], in_=bank[:].rearrange("p (u gx j) -> p gx j u", u=2, gx=4))
 
         def quant_w(t, g):
             cols = slice(1024 * (2 * t + g), 1024 * (2 * t + g + 1))
@@ -218,20 +254,23 @@ def tile_linearattention_pa_kernel(tc, x_bytes, x_scale, wq, wk, out_0, out_1):
                 stop=stop,
             )
 
-        def mm(t, i, three):
-            tb = accp.tile([P, 512], F32, name="tb")
-            ta = accp.tile([P, 512], F32, name="ta")
+        def mm(n):
+            t, i = n // 8, n % 8
+            tb, ta = new_bank(), new_bank()
             for x, bank in ((0, tb), (1, ta)):
                 mx(bank, t, i, 0, x, True, False)
                 mx(bank, t, i, 1, x, False, True)
-            if not three:
-                return tb, ta, None
-            uu = uup.tile([P, 512], F32, name="uu")
+            if n in PLAIN:
+                banks[n] = (tb, ta, None)
+                return
+            uu = new_bank()
             mx(uu, t, i, 0, 0, True, False)
             mx(uu, t, i, 0, 1, False, False)
             mx(uu, t, i, 1, 0, False, False)
             mx(uu, t, i, 1, 1, False, True)
-            return tb, ta, uu
+            banks[n] = (tb, ta, uu)
+
+        banks = {}
 
         def by_heads(ap):
             return ap.rearrange("p (h j) -> p h j", j=64)
@@ -247,8 +286,8 @@ def tile_linearattention_pa_kernel(tc, x_bytes, x_scale, wq, wk, out_0, out_1):
                 op0=ALU.mult, op1=ALU.mult,
             )
 
-        def first_products(i, banks):
-            tb, ta, uu = banks
+        def first_products(i, unit_banks):
+            tb, ta, uu = unit_banks
             kk = p3.tile([P, 2, 512], F32, name="kk")
             if uu is None:
                 k2 = p2.tile([P, 2, 512], F32, name="k2")
@@ -260,8 +299,8 @@ def tile_linearattention_pa_kernel(tc, x_bytes, x_scale, wq, wk, out_0, out_1):
             mult_root2(kk[:, 1, :], ta, ttab[:, i, 1])
             return kk, None
 
-        def last_product(i, banks, k2):
-            tb, ta, uu = banks
+        def last_product(i, unit_banks, k2):
+            tb, ta, uu = unit_banks
             if uu is None:
                 mult(k2[:, 0, :], ta, ctab[:, i, 0])
                 return k2[:]
@@ -298,33 +337,15 @@ def tile_linearattention_pa_kernel(tc, x_bytes, x_scale, wq, wk, out_0, out_1):
                 scalar1=0.0,
             )
 
-        with tc.psum_pool(name="tp1", bufs=4) as tp1:
-            spread_scales(tp1)
-            turn_w(tp1, 0, 0)
-            turn_w(tp1, 0, 1)
-            for q in range(4):
-                xws = [widen(2 * q), widen(2 * q + 1)]
-                turn_x(tp1, 2 * q, xws[0])
-                turn_x(tp1, 2 * q + 1, xws[1])
-                if q < 3:
-                    turn_w(tp1, 0, 2 * q + 2)
-                    turn_w(tp1, 0, 2 * q + 3)
-            quant_x(0)
-            quant_w(0, 0)
-            quant_w(0, 1)
-            quant_x(1)
-            for h in range(4):
-                turn_w(tp1, 1, h)
-            first_banks = [mm(0, 0, False), mm(0, 1, False)]
-            for h in range(4, 8):
-                turn_w(tp1, 1, h)
-        uup = ctx.enter_context(tc.psum_pool(name="uup", bufs=2))
-
         whole = ((0, 8),)
         halves = ((0, 4), (4, 8))
         osts = {}
+        done = set()
+        waiting = []
+        summed = []
 
-        def finish(n, sm):
+        def finish():
+            n, sm = summed.pop(0)
             t, i = n // 8, n % 8
             relu(sm, osts[n // 2][:, :, n % 2, :], 0, 8)
             done.add(n)
@@ -334,31 +355,134 @@ def tile_linearattention_pa_kernel(tc, x_bytes, x_scale, wq, wk, out_0, out_1):
                 i0 = i - n % 2
                 nc.sync.dma_start(out=outv[t][:, :, i0:i0 + 2, :], in_=osts[n // 2][:])
 
-        done = set()
-        waiting = []
-        for n in range(16):
-            t, i = n // 8, n % 8
+        def unit(n):
+            i = n % 8
             if n % 2 == 0:
                 ost = p2.tile([P, 8, 2, P], F32, name="ost")
                 osts[n // 2] = ost
-            banks = first_banks[n] if n < 2 else mm(t, i, n >= PLAIN_UNITS)
-            kk, k2 = first_products(i, banks)
+            kk, k2 = first_products(i, banks[n])
             if n == 15:
                 m, kkm, om = waiting.pop()
-                finish(m, add_v(kkm, om, whole))
-            other = last_product(i, banks, k2)
+                summed.append((m, add_v(kkm, om, whole)))
+            other = last_product(i, banks[n], k2)
             if waiting:
                 m, kkm, om = waiting.pop()
-                finish(m, add_v(kkm, om, whole))
-                if m == 3:
-                    quant_w(1, 0)
-                    quant_w(1, 1)
+                summed.append((m, add_v(kkm, om, whole)))
             if n == 15:
+                while summed:
+                    finish()
                 sm = add_v(kk, other, halves)
                 for h0, h1 in halves:
                     (relu if h0 == 0 else relu_v)(sm, osts[7][:, :, 1, :], h0, h1)
-                    nc.sync.dma_start(out=outv[t][:, h0:h1, i, :], in_=osts[7][:, h0:h1, 1, :])
-            elif n % 3 == 0 or n == 14:
+                    nc.sync.dma_start(out=outv[1][:, h0:h1, i, :], in_=osts[7][:, h0:h1, 1, :])
+            elif n in VECTOR_ADDS:
                 waiting.append((n, kk, other))
             else:
-                finish(n, add_g(kk, other))
+                summed.append((n, add_g(kk, other)))
+
+        spread_scales()
+        turn_w(0, 0)
+        turn_w(0, 1)
+        turn_w(0, 2)
+        turn_w(0, 3)
+        widen(0)
+        turn_x(0)
+        turn_w(0, 4)
+        widen(1)
+        turn_x(1)
+        turn_w(0, 5)
+        widen(2)
+        turn_x(2)
+        turn_w(0, 6)
+        widen(3)
+        turn_x(3)
+        turn_w(0, 7)
+        widen(4)
+        widen(5)
+        quant_x(0)
+        turn_x(4)
+        turn_x(5)
+        cast_x(6)
+        turn_unscaled(6)
+        rope_tables()
+        quant_w(0, 0)
+        quant_w(0, 1)
+        mm(0)
+        scale_x(6)
+        unit(0)
+        while len(summed) > 2:
+            finish()
+        mm(1)
+        unit(1)
+        cast_x(7)
+        turn_unscaled(7)
+        scale_x(7)
+        while len(summed) > 2:
+            finish()
+        mm(2)
+        unit(2)
+        quant_x(1)
+        while len(summed) > 2:
+            finish()
+        turn_w(1, 0)
+        turn_w(1, 1)
+        turn_w(1, 2)
+        turn_w(1, 3)
+        mm(3)
+        unit(3)
+        while len(summed) > 2:
+            finish()
+        turn_w(1, 4)
+        turn_w(1, 5)
+        turn_w(1, 6)
+        turn_w(1, 7)
+        mm(4)
+        unit(4)
+        quant_w(1, 0)
+        while len(summed) > 2:
+            finish()
+        mm(5)
+        unit(5)
+        quant_w(1, 1)
+        while len(summed) > 2:
+            finish()
+        mm(6)
+        unit(6)
+        while len(summed) > 2:
+            finish()
+        mm(7)
+        unit(7)
+        while len(summed) > 2:
+            finish()
+        mm(8)
+        unit(8)
+        while len(summed) > 2:
+            finish()
+        mm(9)
+        unit(9)
+        while len(summed) > 2:
+            finish()
+        mm(10)
+        unit(10)
+        while len(summed) > 2:
+            finish()
+        mm(11)
+        unit(11)
+        while len(summed) > 2:
+            finish()
+        mm(12)
+        unit(12)
+        while len(summed) > 2:
+            finish()
+        mm(13)
+        unit(13)
+        while len(summed) > 2:
+            finish()
+        mm(14)
+        unit(14)
+        while len(summed) > 2:
+            finish()
+        mm(15)
+        unit(15)
+        while len(summed) > 2:
+            finish()

@@ -19,7 +19,7 @@ ACT = mybir.ActivationFunctionType
 P = 128
 TWO_PI = 2.0 * math.pi
 VECTOR_ADDS = (4, 5, 8, 11, 14)
-PLAIN = (0, 2, 3)
+PLAIN = (0, 2, 3, 8, 10, 11)
 PLAIN_UNITS = 4
 
 
@@ -50,8 +50,7 @@ def tile_linearattention_pa_kernel(tc, x_bytes, x_scale, wq, wk, out_0, out_1):
 
         def load_w(rt):
             src = wq if rt < 8 else wk
-            r0 = 128 * (rt % 8)
-            nc.sync.dma_start(out=wraw[rt][:], in_=src[r0:r0 + 128, :])
+            nc.sync.dma_start(out=wraw[rt][:], in_=src.rearrange("(q p i) k -> q i p k", q=4, i=2)[rt % 8 // 2, rt % 2])
 
         load_x(0)
         nc.scalar.dma_start(out=sct[:], in_=x_scale[0].rearrange("o (g p t) -> p (o g) t", g=2, t=4))
@@ -77,9 +76,6 @@ def tile_linearattention_pa_kernel(tc, x_bytes, x_scale, wq, wk, out_0, out_1):
 
         ident = const.tile([P, P], F32, name="ident")
         masks.make_identity(nc, ident[:])
-        perm = const.tile([P, P], F32, name="perm")
-        nc.scalar.copy(out=perm[:, 0:64], in_=ident[:, 1:128:2])
-        nc.scalar.copy(out=perm[:, 64:128], in_=ident[:, 0:128:2])
 
         abc = const.tile([P, 12], F32, name="abc")
         nc.vector.memset(abc[:], 1.0)
@@ -161,12 +157,12 @@ def tile_linearattention_pa_kernel(tc, x_bytes, x_scale, wq, wk, out_0, out_1):
             bank = psum.tile([P, 512], F32, name="bank")
             return bank
 
-        def turn(words, eye, u_major):
+        def turn(words):
             bank = new_bank()
             for g in range(2):
                 for u in range(2):
-                    slot = 2 * u + g if u_major else 2 * g + u
-                    nc.tensor.transpose(bank[:, P * slot:P * (slot + 1)], words[:, 256 * g + u:256 * (g + 1):2], eye[:])
+                    slot = 2 * g + u
+                    nc.tensor.transpose(bank[:, P * slot:P * (slot + 1)], words[:, 256 * g + u:256 * (g + 1):2], ident[:])
             return bank
 
         def spread_scales():
@@ -198,7 +194,7 @@ def tile_linearattention_pa_kernel(tc, x_bytes, x_scale, wq, wk, out_0, out_1):
             xws[i] = xw
 
         def turn_unscaled(i):
-            xbanks[i] = turn(xws[i][:].bitcast(F32), ident, False)
+            xbanks[i] = turn(xws[i][:].bitcast(F32))
 
         def scale_x(i):
             if i % 4 == 0:
@@ -218,7 +214,7 @@ def tile_linearattention_pa_kernel(tc, x_bytes, x_scale, wq, wk, out_0, out_1):
                 xg = p2.tile([P, 4096], BF16, name="xg", align_bytes=64)
                 xgs[i // 4] = xg
             xgw = xgs[i // 4][:].bitcast(F32).rearrange("p (i g r u) -> p i g r u", i=4, g=2, u=2)
-            bank = turn(xws[i][:].bitcast(F32), ident, False)
+            bank = turn(xws[i][:].bitcast(F32))
             nc.scalar.copy(out=xgw[:, i % 4], in_=bank[:].rearrange("p (g u r) -> p g r u", g=2, u=2))
 
         def quant_x(q):
@@ -227,13 +223,14 @@ def tile_linearattention_pa_kernel(tc, x_bytes, x_scale, wq, wk, out_0, out_1):
 
         wgs = {}
 
-        def turn_w(t, h):
-            if h == 0:
+        def turn_w(t, m):
+            if m == 0:
                 wg = p2.tile([P, 8192], BF16, name="wg", align_bytes=64)
                 wgs[t] = wg
-            wgw = wgs[t][:].bitcast(F32).rearrange("p (gx h j u) -> p gx h j u", gx=4, h=8, u=2)
-            bank = turn(wraw[8 * t + h][:].bitcast(F32), perm, True)
-            nc.scalar.copy(out=wgw[:, :, h], in_=bank[:].rearrange("p (u gx j) -> p gx j u", u=2, gx=4))
+            q, i = m // 2, m % 2
+            wgw = wgs[t][:].bitcast(F32).rearrange("p (g x q c u) -> p g x q c u", g=2, x=2, q=4, u=2)
+            bank = turn(wraw[8 * t + m][:].bitcast(F32))
+            nc.scalar.copy(out=wgw[:, :, 1 - i, q], in_=bank[:].rearrange("p (g u c) -> p g c u", g=2, u=2))
 
         def quant_w(t, g):
             cols = slice(1024 * (2 * t + g), 1024 * (2 * t + g + 1))

@@ -18,8 +18,8 @@ ACT = mybir.ActivationFunctionType
 
 P = 128
 TWO_PI = 2.0 * math.pi
-VECTOR_ADDS = (4, 5, 8, 11, 14)
-PLAIN = (0, 2, 3, 8, 10, 11)
+VECTOR_PARTS = {5: (0, 1), 8: (0, 1), 11: (0, 1), 14: (1,)}
+PLAIN = (0, 2, 3)
 PLAIN_UNITS = 4
 
 
@@ -30,7 +30,7 @@ def tile_linearattention_pa_kernel(tc, x_bytes, x_scale, wq, wk, out_0, out_1):
         const = ctx.enter_context(tc.tile_pool(name="const", bufs=1))
         p2 = ctx.enter_context(tc.tile_pool(name="p2", bufs=2))
         p3 = ctx.enter_context(tc.tile_pool(name="p3", bufs=5))
-        p8 = ctx.enter_context(tc.tile_pool(name="p8", bufs=8))
+        p4 = ctx.enter_context(tc.tile_pool(name="p4", bufs=4))
         psum = ctx.enter_context(tc.psum_pool(name="psum", bufs=8))
 
         xv = x_bytes[0].rearrange("(p i) k -> p (i k)", i=8)
@@ -178,7 +178,7 @@ def tile_linearattention_pa_kernel(tc, x_bytes, x_scale, wq, wk, out_0, out_1):
         xgs = {}
 
         def widen(i):
-            xw = p8.tile([P, 1024], BF16, name="xw")
+            xw = p4.tile([P, 1024], BF16, name="xw")
             lo = 1024 * (i % 2)
             nc.vector.tensor_tensor(
                 out=xw[:], in0=xby[i // 2][:, lo:lo + 1024].bitcast(FP8), in1=xsc[:], op=ALU.mult
@@ -188,7 +188,7 @@ def tile_linearattention_pa_kernel(tc, x_bytes, x_scale, wq, wk, out_0, out_1):
         xbanks = {}
 
         def cast_x(i):
-            xw = p8.tile([P, 1024], BF16, name="xw")
+            xw = p4.tile([P, 1024], BF16, name="xw")
             lo = 1024 * (i % 2)
             nc.scalar.copy(out=xw[:], in_=xby[i // 2][:, lo:lo + 1024].bitcast(FP8))
             xws[i] = xw
@@ -307,18 +307,8 @@ def tile_linearattention_pa_kernel(tc, x_bytes, x_scale, wq, wk, out_0, out_1):
 
         outv = [o[0].rearrange("h (p i) d -> p h i d", i=8) for o in (out_0, out_1)]
 
-        def add_v(kk, other, hs):
-            sm = p3.tile([P, 2, 512], F32, name="sm")
-            for h0, h1 in hs:
-                cols = slice(64 * h0, 64 * h1)
-                nc.vector.tensor_tensor(out=sm[:, :, cols], in0=kk[:, :, cols], in1=other[:, :, cols], op=ALU.add)
-            return sm
-
-        def add_g(kk, other):
-            sm = p3.tile([P, 2, 512], F32, name="sm")
-            for x in range(2):
-                nc.gpsimd.tensor_tensor(out=sm[:, x, :], in0=kk[:, x, :], in1=other[:, x, :], op=ALU.add)
-            return sm
+        def add(engine, sm, kk, other, x, cols=slice(0, 512)):
+            engine.tensor_tensor(out=sm[:, x, cols], in0=kk[:, x, cols], in1=other[:, x, cols], op=ALU.add)
 
         def relu(sm, dst, h0, h1):
             nc.scalar.activation(
@@ -334,7 +324,6 @@ def tile_linearattention_pa_kernel(tc, x_bytes, x_scale, wq, wk, out_0, out_1):
                 scalar1=0.0,
             )
 
-        whole = ((0, 8),)
         halves = ((0, 4), (4, 8))
         osts = {}
         done = set()
@@ -352,30 +341,41 @@ def tile_linearattention_pa_kernel(tc, x_bytes, x_scale, wq, wk, out_0, out_1):
                 i0 = i - n % 2
                 nc.sync.dma_start(out=outv[t][:, :, i0:i0 + 2, :], in_=osts[n // 2][:])
 
+        def vector_adds():
+            if waiting:
+                m, sm, kk, other, parts = waiting.pop()
+                if len(parts) == 2:
+                    nc.vector.tensor_tensor(out=sm[:], in0=kk[:], in1=other, op=ALU.add)
+                else:
+                    add(nc.vector, sm, kk, other, 1)
+                summed.append((m, sm))
+
         def unit(n):
             i = n % 8
             if n % 2 == 0:
-                ost = p2.tile([P, 8, 2, P], F32, name="ost")
+                ost = p4.tile([P, 8, 2, P], F32, name="ost")
                 osts[n // 2] = ost
             kk, k2 = first_products(i, banks[n])
-            if n == 15:
-                m, kkm, om = waiting.pop()
-                summed.append((m, add_v(kkm, om, whole)))
             other = last_product(i, banks[n], k2)
-            if waiting:
-                m, kkm, om = waiting.pop()
-                summed.append((m, add_v(kkm, om, whole)))
+            sm = p3.tile([P, 2, 512], F32, name="sm")
+            vector_adds()
             if n == 15:
                 while summed:
                     finish()
-                sm = add_v(kk, other, halves)
                 for h0, h1 in halves:
+                    cols = slice(64 * h0, 64 * h1)
+                    nc.vector.tensor_tensor(out=sm[:, :, cols], in0=kk[:, :, cols], in1=other[:, :, cols], op=ALU.add)
                     (relu if h0 == 0 else relu_v)(sm, osts[7][:, :, 1, :], h0, h1)
                     nc.sync.dma_start(out=outv[1][:, h0:h1, i, :], in_=osts[7][:, h0:h1, 1, :])
-            elif n in VECTOR_ADDS:
-                waiting.append((n, kk, other))
+                return
+            mine = VECTOR_PARTS.get(n, ())
+            for x in range(2):
+                if x not in mine:
+                    add(nc.gpsimd, sm, kk, other, x)
+            if mine:
+                waiting.append((n, sm, kk, other, mine))
             else:
-                summed.append((n, add_g(kk, other)))
+                summed.append((n, sm))
 
         spread_scales()
         turn_w(0, 0)

@@ -18,9 +18,9 @@ ACT = mybir.ActivationFunctionType
 
 P = 128
 TWO_PI = 2.0 * math.pi
-VECTOR_PARTS = {5: (0, 1), 8: (0, 1), 11: (0, 1), 14: (1,)}
-PLAIN = (0, 2, 3)
-PLAIN_UNITS = 4
+VECTOR_PARTS = {2: (0, 1), 5: (0, 1), 8: (0, 1), 11: (0, 1), 14: (0, 1)}
+PLAIN = (0, 1)
+PLAIN_UNITS = 2
 
 
 def tile_linearattention_pa_kernel(tc, x_bytes, x_scale, wq, wk, out_0, out_1):
@@ -54,15 +54,25 @@ def tile_linearattention_pa_kernel(tc, x_bytes, x_scale, wq, wk, out_0, out_1):
 
         load_x(0)
         nc.scalar.dma_start(out=sct[:], in_=x_scale[0].rearrange("o (g p t) -> p (o g) t", g=2, t=4))
+        load_x(1)
         load_w(0)
         load_w(1)
-        load_x(1)
-        for rt in range(2, 8):
-            load_w(rt)
+        load_w(2)
+        load_w(3)
         load_x(2)
+        load_w(4)
+        load_w(5)
         load_x(3)
-        for rt in range(8, 16):
-            load_w(rt)
+        load_w(6)
+        load_w(7)
+        load_w(8)
+        load_w(9)
+        load_w(10)
+        load_w(11)
+        load_w(12)
+        load_w(13)
+        load_w(14)
+        load_w(15)
 
         posf = const.tile([P, 8, 1], F32, name="posf")
         nc.gpsimd.iota(
@@ -185,30 +195,6 @@ def tile_linearattention_pa_kernel(tc, x_bytes, x_scale, wq, wk, out_0, out_1):
             )
             xws[i] = xw
 
-        xbanks = {}
-
-        def cast_x(i):
-            xw = p4.tile([P, 1024], BF16, name="xw")
-            lo = 1024 * (i % 2)
-            nc.scalar.copy(out=xw[:], in_=xby[i // 2][:, lo:lo + 1024].bitcast(FP8))
-            xws[i] = xw
-
-        def turn_unscaled(i):
-            xbanks[i] = turn(xws[i][:].bitcast(F32))
-
-        def scale_x(i):
-            if i % 4 == 0:
-                xg = p2.tile([P, 4096], BF16, name="xg", align_bytes=64)
-                xgs[i // 4] = xg
-            for g in range(2):
-                lo = 1024 * (i % 4) + 512 * g
-                nc.vector.tensor_tensor(
-                    out=xgs[i // 4][:, lo:lo + 512].rearrange("p (r u e) -> p r u e", u=2, e=2),
-                    in0=xbanks[i][:, 256 * g:256 * (g + 1)].bitcast(BF16).rearrange("p (u r e) -> p r u e", u=2, e=2),
-                    in1=sct[:, g, :].rearrange("p (o u e) -> p o u e", o=1, e=2).to_broadcast([P, P, 2, 2]),
-                    op=ALU.mult,
-                )
-
         def turn_x(i):
             if i % 4 == 0:
                 xg = p2.tile([P, 4096], BF16, name="xg", align_bytes=64)
@@ -217,9 +203,12 @@ def tile_linearattention_pa_kernel(tc, x_bytes, x_scale, wq, wk, out_0, out_1):
             bank = turn(xws[i][:].bitcast(F32))
             nc.scalar.copy(out=xgw[:, i % 4], in_=bank[:].rearrange("p (g u r) -> p g r u", g=2, u=2))
 
-        def quant_x(q):
-            cols = slice(1024 * q, 1024 * (q + 1))
-            nc.vector.quantize_mx(out=xcodes[:, cols].bitcast(FP8X4), scales=xscl[:, cols], in_=xgs[q][:])
+        def quant_x(i0, i1):
+            cols = slice(256 * i0, 256 * i1)
+            lo = 1024 * (i0 % 4)
+            nc.vector.quantize_mx(
+                out=xcodes[:, cols].bitcast(FP8X4), scales=xscl[:, cols], in_=xgs[i0 // 4][:, lo:lo + 1024 * (i1 - i0)]
+            )
 
         wgs = {}
 
@@ -379,68 +368,66 @@ def tile_linearattention_pa_kernel(tc, x_bytes, x_scale, wq, wk, out_0, out_1):
 
         spread_scales()
         turn_w(0, 0)
-        turn_w(0, 1)
-        turn_w(0, 2)
-        turn_w(0, 3)
         widen(0)
         turn_x(0)
-        turn_w(0, 4)
+        turn_w(0, 1)
         widen(1)
         turn_x(1)
-        turn_w(0, 5)
+        turn_w(0, 2)
         widen(2)
         turn_x(2)
-        turn_w(0, 6)
+        turn_w(0, 3)
         widen(3)
         turn_x(3)
-        turn_w(0, 7)
+        turn_w(0, 4)
         widen(4)
-        widen(5)
-        quant_x(0)
         turn_x(4)
+        turn_w(0, 5)
+        widen(5)
         turn_x(5)
-        cast_x(6)
-        turn_unscaled(6)
+        turn_w(0, 6)
+        widen(6)
+        turn_x(6)
+        turn_w(0, 7)
+        widen(7)
+        turn_x(7)
         rope_tables()
+        quant_x(0, 4)
         quant_w(0, 0)
         quant_w(0, 1)
+        turn_w(1, 0)
+        turn_w(1, 1)
+        turn_w(1, 2)
+        turn_w(1, 3)
+        quant_x(4, 8)
         mm(0)
-        scale_x(6)
         unit(0)
         while len(summed) > 2:
             finish()
         mm(1)
         unit(1)
-        cast_x(7)
-        turn_unscaled(7)
-        scale_x(7)
         while len(summed) > 2:
             finish()
         mm(2)
-        unit(2)
-        quant_x(1)
-        while len(summed) > 2:
-            finish()
-        turn_w(1, 0)
-        turn_w(1, 1)
-        turn_w(1, 2)
-        turn_w(1, 3)
-        mm(3)
-        unit(3)
-        while len(summed) > 2:
-            finish()
         turn_w(1, 4)
         turn_w(1, 5)
         turn_w(1, 6)
         turn_w(1, 7)
+        unit(2)
+        quant_w(1, 0)
+        quant_w(1, 1)
+        while len(summed) > 2:
+            finish()
+        mm(3)
+        unit(3)
+        while len(summed) > 2:
+            finish()
         mm(4)
         unit(4)
-        quant_w(1, 0)
         while len(summed) > 2:
             finish()
         mm(5)
         unit(5)
-        quant_w(1, 1)
         while len(summed) > 2:
             finish()
         mm(6)

@@ -190,9 +190,11 @@ def tile_linearattention_pa_kernel(tc, x_bytes, x_scale, wq, wk, out_0, out_1):
         def widen(i):
             xw = p4.tile([P, 1024], BF16, name="xw")
             lo = 1024 * (i % 2)
-            nc.vector.tensor_tensor(
-                out=xw[:], in0=xby[i // 2][:, lo:lo + 1024].bitcast(FP8), in1=xsc[:], op=ALU.mult
-            )
+            step = 512 if i == 0 else 1024
+            for c in range(0, 1024, step):
+                nc.vector.tensor_tensor(
+                    out=xw[:, c:c + step], in0=xby[i // 2][:, lo + c:lo + c + step].bitcast(FP8), in1=xsc[:, c:c + step], op=ALU.mult
+                )
             xws[i] = xw
 
         def turn_x(i):
@@ -345,12 +347,14 @@ def tile_linearattention_pa_kernel(tc, x_bytes, x_scale, wq, wk, out_0, out_1):
                 ost = p4.tile([P, 8, 2, P], F32, name="ost")
                 osts[n // 2] = ost
             kk, k2 = first_products(i, banks[n])
+            if n == 15:
+                vector_adds()
+                while summed:
+                    finish()
             other = last_product(i, banks[n], k2)
             sm = p3.tile([P, 2, 512], F32, name="sm")
             vector_adds()
             if n == 15:
-                while summed:
-                    finish()
                 for h0, h1 in halves:
                     cols = slice(64 * h0, 64 * h1)
                     nc.vector.tensor_tensor(out=sm[:, :, cols], in0=kk[:, :, cols], in1=other[:, :, cols], op=ALU.add)

@@ -372,27 +372,27 @@ def tile_linearattention_pa_kernel(tc, x_bytes, x_scale, wq, wk, out_0, out_1):
 
         spread_scales()
         turn_w(0, 0)
+        turn_w(0, 1)
+        turn_w(0, 2)
+        turn_w(0, 3)
         widen(0)
         turn_x(0)
-        turn_w(0, 1)
+        turn_w(0, 4)
         widen(1)
         turn_x(1)
-        turn_w(0, 2)
+        turn_w(0, 5)
         widen(2)
         turn_x(2)
-        turn_w(0, 3)
+        turn_w(0, 6)
         widen(3)
         turn_x(3)
-        turn_w(0, 4)
+        turn_w(0, 7)
         widen(4)
         turn_x(4)
-        turn_w(0, 5)
         widen(5)
         turn_x(5)
-        turn_w(0, 6)
         widen(6)
         turn_x(6)
-        turn_w(0, 7)
         widen(7)
         turn_x(7)
         rope_tables()
@@ -409,14 +409,14 @@ def tile_linearattention_pa_kernel(tc, x_bytes, x_scale, wq, wk, out_0, out_1):
         while len(summed) > 2:
             finish()
         mm(1)
-        unit(1)
-        while len(summed) > 2:
-            finish()
-        mm(2)
         turn_w(1, 4)
         turn_w(1, 5)
         turn_w(1, 6)
         turn_w(1, 7)
+        unit(1)
+        while len(summed) > 2:
+            finish()
+        mm(2)
         unit(2)
         quant_w(1, 0)
         quant_w(1, 1)

from contextlib import ExitStack
import math

import concourse.masks as masks
import concourse.mybir as mybir

FLOPS = 2 * 1024 * 1024 * 2048

F32 = mybir.dt.float32
BF16 = mybir.dt.bfloat16
U32 = mybir.dt.uint32
U8 = mybir.dt.uint8
I32 = mybir.dt.int32
FP8 = mybir.dt.float8_e4m3fn
FP8X4 = mybir.dt.float8_e4m3fn_x4
ALU = mybir.AluOpType
ACT = mybir.ActivationFunctionType

P = 128
TWO_PI = 2.0 * math.pi
VECTOR_PARTS = {2: (0, 1), 5: (0, 1), 8: (0, 1), 11: (0, 1), 14: (0, 1)}
PLAIN = (0, 1)
PLAIN_UNITS = 2


def tile_linearattention_pa_kernel(tc, x_bytes, x_scale, wq, wk, out_0, out_1):
    nc = tc.nc
    with ExitStack() as ctx:
        ctx.enter_context(tc.manual_schedule(engines={mybir.EngineType.DVE, mybir.EngineType.PE, mybir.EngineType.Activation}))
        const = ctx.enter_context(tc.tile_pool(name="const", bufs=1))
        p2 = ctx.enter_context(tc.tile_pool(name="p2", bufs=2))
        p3 = ctx.enter_context(tc.tile_pool(name="p3", bufs=5))
        p4 = ctx.enter_context(tc.tile_pool(name="p4", bufs=4))
        psum = ctx.enter_context(tc.psum_pool(name="psum", bufs=8))

        xv = x_bytes[0].rearrange("(p i) k -> p (i k)", i=8)
        xby = []
        for q in range(4):
            xbq = const.tile([P, 2048], U8, name="xbytes%d" % q)
            xby.append(xbq)
        sct = const.tile([P, 2, 4], F32, name="sct")
        xsc = const.tile([P, 1024], F32, name="xsc")
        wraw = []
        for rt in range(16):
            wr = const.tile([P, 1024], BF16, name="wraw%d" % rt)
            wraw.append(wr)

        def load_x(q):
            nc.sync.dma_start(out=xby[q][:], in_=xv[:, 2048 * q:2048 * (q + 1)])

        def load_w(rt):
            src = wq if rt < 8 else wk
            nc.sync.dma_start(out=wraw[rt][:], in_=src.rearrange("(q p i) k -> q i p k", q=4, i=2)[rt % 8 // 2, rt % 2])

        load_x(0)
        nc.scalar.dma_start(out=sct[:], in_=x_scale[0].rearrange("o (g p t) -> p (o g) t", g=2, t=4))
        load_x(1)
        load_w(0)
        load_w(1)
        load_w(2)
        load_w(3)
        load_x(2)
        load_w(4)
        load_w(5)
        load_x(3)
        load_w(6)
        load_w(7)
        load_w(8)
        load_w(9)
        load_w(10)
        load_w(11)
        load_w(12)
        load_w(13)
        load_w(14)
        load_w(15)

        posf = const.tile([P, 8, 1], F32, name="posf")
        nc.gpsimd.iota(
            posf[:].rearrange("p i o -> p (i o)"), pattern=[[1, 8]], base=0, channel_multiplier=8,
            allow_small_or_imprecise_dtypes=True,
        )
        one = const.tile([P, 1], F32, name="one")
        nc.gpsimd.memset(one[:], 1.0)
        warm = const.tile([P, 1], F32, name="warm")
        nc.scalar.activation(out=warm[:], in_=one[:], func=ACT.Sin)

        ident = const.tile([P, P], F32, name="ident")
        masks.make_identity(nc, ident[:])

        abc = const.tile([P, 12], F32, name="abc")
        nc.vector.memset(abc[:], 1.0)
        for b in range(2):
            for f in range(3):
                half = abc[:, 4 * f:4 * f + 4].rearrange("p (a two l) -> p a two l", two=2, l=1 << b)[:, :, 1, :]
                nc.vector.tensor_scalar_mul(out=half, in0=half, scalar1=10000.0 ** (-((16, 4, 1)[f] << b) / 64.0))
        bc = const.tile([P, 4, 4], F32, name="bc")
        nc.vector.tensor_tensor(
            out=bc[:], in0=abc[:, 4:8].unsqueeze(2).to_broadcast([P, 4, 4]),
            in1=abc[:, 8:12].unsqueeze(1).to_broadcast([P, 4, 4]), op=ALU.mult,
        )
        pa = const.tile([P, 8, 4], F32, name="pa")
        nc.vector.scalar_tensor_tensor(
            out=pa[:], in0=posf[:].to_broadcast([P, 8, 4]), scalar=1.0 / TWO_PI,
            in1=abc[:, 0:4].unsqueeze(1).to_broadcast([P, 8, 4]), op0=ALU.mult, op1=ALU.mult,
        )
        tau = const.tile([P, 32, 16], F32, name="tau")
        ki = const.tile([P, 512], I32, name="ki")
        fr = const.tile([P, 512], F32, name="fr")
        ng = const.tile([P, 8, 64], F32, name="ng")
        ab = const.tile([P, 8, 64], F32, name="ab")
        tauf = tau[:].rearrange("p r q -> p (r q)")
        ngf = ng[:].rearrange("p i j -> p (i j)")
        abf = ab[:].rearrange("p i j -> p (i j)")
        table_halves = (slice(0, 256), slice(256, 512))
        for z in range(2):
            nc.vector.tensor_tensor(
                out=tau[:, 16 * z:16 * z + 16, :],
                in0=pa[:].rearrange("p i a -> p (i a)")[:, 16 * z:16 * z + 16].unsqueeze(2).to_broadcast([P, 16, 16]),
                in1=bc[:].rearrange("p b c -> p (b c)").unsqueeze(1).to_broadcast([P, 16, 16]), op=ALU.mult,
            )
        for cols in table_halves:
            nc.vector.tensor_copy(out=ki[:, cols], in_=tauf[:, cols])
        for cols in table_halves:
            nc.vector.tensor_tensor(out=fr[:, cols], in0=tauf[:, cols], in1=ki[:, cols], op=ALU.subtract)
        for cols in table_halves:
            nc.vector.scalar_tensor_tensor(
                out=ngf[:, cols], in0=fr[:, cols], scalar=0.5, in1=fr[:, cols], op0=ALU.is_gt, op1=ALU.subtract
            )
        for cols in table_halves:
            nc.vector.scalar_tensor_tensor(
                out=abf[:, cols], in0=ngf[:, cols], scalar=-1.0, in1=ngf[:, cols], op0=ALU.mult, op1=ALU.max
            )
        for cols in table_halves:
            nc.vector.scalar_tensor_tensor(
                out=tauf[:, cols], in0=ngf[:, cols], scalar=-0.375, in1=ngf[:, cols], op0=ALU.is_lt, op1=ALU.add
            )
        for cols in table_halves:
            nc.vector.scalar_tensor_tensor(
                out=fr[:, cols], in0=ngf[:, cols], scalar=0.375, in1=ngf[:, cols], op0=ALU.is_gt, op1=ALU.subtract
            )

        ctab = const.tile([P, 8, 1, 1, 64], F32, name="ctab")
        ttab = const.tile([P, 8, 2, 1, 64], F32, name="ttab")
        tview = ttab[:].rearrange("p i x o j -> p i x (o j)")
        stab = const.tile([P, PLAIN_UNITS, 2, 1, 64], F32, name="stab")
        sview = stab[:].rearrange("p i x o j -> p i x (o j)")

        def rope_tables():
            nc.scalar.activation(
                out=ctab[:].rearrange("p i a b j -> p i (a b j)"), in_=ab[:], func=ACT.Sin, bias=math.pi / 2.0, scale=-TWO_PI
            )
            nc.scalar.activation(out=sview[:, :, 0, :], in_=ng[:, 0:PLAIN_UNITS, :], func=ACT.Sin, scale=TWO_PI)
            nc.scalar.activation(out=sview[:, :, 1, :], in_=ng[:, 0:PLAIN_UNITS, :], func=ACT.Sin, scale=-TWO_PI)
            nc.scalar.activation(
                out=tview[:, :, 0, :], in_=tauf.rearrange("p (i j) -> p i j", j=64), func=ACT.Sin, bias=-math.pi / 4.0, scale=TWO_PI
            )
            nc.scalar.activation(
                out=tview[:, :, 1, :], in_=fr[:].rearrange("p (i j) -> p i j", j=64), func=ACT.Sin, bias=-math.pi / 4.0, scale=TWO_PI
            )

        xcodes = const.tile([P, 2048], U32, name="xcodes", align_bytes=64)
        xscl = const.tile([P, 2048], U8, name="xscl", align_bytes=64)
        wcodes = const.tile([P, 4096], U32, name="wcodes", align_bytes=64)
        wscl = const.tile([P, 4096], U8, name="wscl", align_bytes=64)

        def new_bank():
            bank = psum.tile([P, 512], F32, name="bank")
            return bank

        def turn(words):
            bank = new_bank()
            for g in range(2):
                for u in range(2):
                    slot = 2 * g + u
                    nc.tensor.transpose(bank[:, P * slot:P * (slot + 1)], words[:, 256 * g + u:256 * (g + 1):2], ident[:])
            return bank

        def spread_scales():
            for g in range(2):
                bank = new_bank()
                for t in range(4):
                    nc.tensor.transpose(bank[:, P * t:P * (t + 1)], sct[:, g, t:t + 1].to_broadcast([P, P]), ident[:])
                nc.scalar.copy(
                    out=xsc[:, 512 * g:512 * (g + 1)].rearrange("p (w t) -> p w t", t=4), in_=bank[:].rearrange("p (t w) -> p w t", t=4)
                )

        xws = {}
        xgs = {}

        def widen(i):
            xw = p4.tile([P, 1024], BF16, name="xw")
            lo = 1024 * (i % 2)
            step = 512 if i == 0 else 1024
            for c in range(0, 1024, step):
                nc.vector.tensor_tensor(
                    out=xw[:, c:c + step], in0=xby[i // 2][:, lo + c:lo + c + step].bitcast(FP8), in1=xsc[:, c:c + step], op=ALU.mult
                )
            xws[i] = xw

        def turn_x(i):
            if i % 4 == 0:
                xg = p2.tile([P, 4096], BF16, name="xg", align_bytes=64)
                xgs[i // 4] = xg
            xgw = xgs[i // 4][:].bitcast(F32).rearrange("p (i g r u) -> p i g r u", i=4, g=2, u=2)
            bank = turn(xws[i][:].bitcast(F32))
            nc.scalar.copy(out=xgw[:, i % 4], in_=bank[:].rearrange("p (g u r) -> p g r u", g=2, u=2))

        def quant_x(i0, i1):
            cols = slice(256 * i0, 256 * i1)
            lo = 1024 * (i0 % 4)
            nc.vector.quantize_mx(
                out=xcodes[:, cols].bitcast(FP8X4), scales=xscl[:, cols], in_=xgs[i0 // 4][:, lo:lo + 1024 * (i1 - i0)]
            )

        wgs = {}

        def turn_w(t, m):
            if m == 0:
                wg = p2.tile([P, 8192], BF16, name="wg", align_bytes=64)
                wgs[t] = wg
            q, i = m // 2, m % 2
            wgw = wgs[t][:].bitcast(F32).rearrange("p (g x q c u) -> p g x q c u", g=2, x=2, q=4, u=2)
            bank = turn(wraw[8 * t + m][:].bitcast(F32))
            nc.scalar.copy(out=wgw[:, :, 1 - i, q], in_=bank[:].rearrange("p (g u c) -> p g c u", g=2, u=2))

        def quant_w(t, g):
            cols = slice(1024 * (2 * t + g), 1024 * (2 * t + g + 1))
            nc.vector.quantize_mx(
                out=wcodes[:, cols].bitcast(FP8X4), scales=wscl[:, cols], in_=wgs[t][:, 4096 * g:4096 * (g + 1)]
            )

        def mx(out, t, i, g, x, start, stop):
            xs = slice(128 * (2 * i + g), 128 * (2 * i + g + 1))
            w0 = 1024 * (2 * t + g) + 512 * x
            nc.tensor.matmul_mx(
                out=out[:],
                lhsT=xcodes[:, xs].bitcast(FP8X4),
                lhsT_scale=xscl[:, xs],
                rhs=wcodes[:, w0:w0 + 512].bitcast(FP8X4),
                rhs_scale=wscl[:, w0:w0 + 512],
                start=start,
                stop=stop,
            )

        def mm(n):
            t, i = n // 8, n % 8
            tb, ta = new_bank(), new_bank()
            for x, bank in ((0, tb), (1, ta)):
                mx(bank, t, i, 0, x, True, False)
                mx(bank, t, i, 1, x, False, True)
            if n in PLAIN:
                banks[n] = (tb, ta, None)
                return
            uu = new_bank()
            mx(uu, t, i, 0, 0, True, False)
            mx(uu, t, i, 0, 1, False, False)
            mx(uu, t, i, 1, 0, False, False)
            mx(uu, t, i, 1, 1, False, True)
            banks[n] = (tb, ta, uu)

        banks = {}

        def by_heads(ap):
            return ap.rearrange("p (h j) -> p h j", j=64)

        def mult(out, bank, table):
            nc.vector.tensor_tensor(
                out=by_heads(out), in0=by_heads(bank[:]), in1=table.to_broadcast([P, 8, 64]), op=ALU.mult
            )

        def mult_root2(out, bank, table):
            nc.vector.scalar_tensor_tensor(
                out=by_heads(out), in0=by_heads(bank[:]), scalar=math.sqrt(2.0), in1=table.to_broadcast([P, 8, 64]),
                op0=ALU.mult, op1=ALU.mult,
            )

        def first_products(i, unit_banks):
            tb, ta, uu = unit_banks
            kk = p3.tile([P, 2, 512], F32, name="kk")
            if uu is None:
                k2 = p2.tile([P, 2, 512], F32, name="k2")
                mult(kk[:, 0, :], tb, stab[:, i, 0])
                mult(k2[:, 1, :], tb, ctab[:, i, 0])
                mult(kk[:, 1, :], ta, stab[:, i, 1])
                return kk, k2
            mult_root2(kk[:, 0, :], tb, ttab[:, i, 0])
            mult_root2(kk[:, 1, :], ta, ttab[:, i, 1])
            return kk, None

        def last_product(i, unit_banks, k2):
            tb, ta, uu = unit_banks
            if uu is None:
                mult(k2[:, 0, :], ta, ctab[:, i, 0])
                return k2[:]
            k1 = p3.tile([P, 1, 512], F32, name="k1")
            mult(k1[:, 0, :], uu, ctab[:, i, 0])
            return k1[:].to_broadcast([P, 2, 512])

        outv = [o[0].rearrange("h (p i) d -> p h i d", i=8) for o in (out_0, out_1)]

        def add(engine, sm, kk, other, x, cols=slice(0, 512)):
            engine.tensor_tensor(out=sm[:, x, cols], in0=kk[:, x, cols], in1=other[:, x, cols], op=ALU.add)

        def relu(sm, dst, h0, h1):
            nc.scalar.activation(
                out=dst[:, h0:h1, :].rearrange("p h (j e) -> p h j e", e=2),
                in_=sm[:, :, 64 * h0:64 * h1].rearrange("p e (h j) -> p h j e", j=64),
                func=ACT.Relu,
            )

        def relu_v(sm, dst, h0, h1):
            nc.vector.tensor_scalar_max(
                out=dst[:, h0:h1, :].rearrange("p h (j e) -> p h j e", e=2),
                in0=sm[:, :, 64 * h0:64 * h1].rearrange("p e (h j) -> p h j e", j=64),
                scalar1=0.0,
            )

        halves = ((0, 4), (4, 8))
        osts = {}
        done = set()
        waiting = []
        summed = []

        def finish():
            n, sm = summed.pop(0)
            t, i = n // 8, n % 8
            relu(sm, osts[n // 2][:, :, n % 2, :], 0, 8)
            done.add(n)
            if n >= 12:
                nc.sync.dma_start(out=outv[t][:, :, i, :], in_=osts[n // 2][:, :, n % 2, :])
            elif (n ^ 1) in done:
                i0 = i - n % 2
                nc.sync.dma_start(out=outv[t][:, :, i0:i0 + 2, :], in_=osts[n // 2][:])

        def vector_adds():
            if waiting:
                m, sm, kk, other, parts = waiting.pop()
                if len(parts) == 2:
                    nc.vector.tensor_tensor(out=sm[:], in0=kk[:], in1=other, op=ALU.add)
                else:
                    add(nc.vector, sm, kk, other, 1)
                summed.append((m, sm))

        def unit(n):
            i = n % 8
            if n % 2 == 0:
                ost = p4.tile([P, 8, 2, P], F32, name="ost")
                osts[n // 2] = ost
            kk, k2 = first_products(i, banks[n])
            if n == 15:
                vector_adds()
                while summed:
                    finish()
            other = last_product(i, banks[n], k2)
            sm = p3.tile([P, 2, 512], F32, name="sm")
            vector_adds()
            if n == 15:
                for h0, h1 in halves:
                    cols = slice(64 * h0, 64 * h1)
                    nc.vector.tensor_tensor(out=sm[:, :, cols], in0=kk[:, :, cols], in1=other[:, :, cols], op=ALU.add)
                    (relu if h0 == 0 else relu_v)(sm, osts[7][:, :, 1, :], h0, h1)
                    nc.sync.dma_start(out=outv[1][:, h0:h1, i, :], in_=osts[7][:, h0:h1, 1, :])
                return
            mine = VECTOR_PARTS.get(n, ())
            for x in range(2):
                if x not in mine:
                    add(nc.gpsimd, sm, kk, other, x)
            if mine:
                waiting.append((n, sm, kk, other, mine))
            else:
                summed.append((n, sm))

        spread_scales()
        turn_w(0, 0)
        turn_w(0, 1)
        turn_w(0, 2)
        turn_w(0, 3)
        widen(0)
        turn_x(0)
        turn_w(0, 4)
        widen(1)
        turn_x(1)
        turn_w(0, 5)
        widen(2)
        turn_x(2)
        turn_w(0, 6)
        widen(3)
        turn_x(3)
        turn_w(0, 7)
        widen(4)
        turn_x(4)
        widen(5)
        turn_x(5)
        widen(6)
        turn_x(6)
        widen(7)
        turn_x(7)
        rope_tables()
        quant_x(0, 4)
        quant_w(0, 0)
        quant_w(0, 1)
        turn_w(1, 0)
        turn_w(1, 1)
        turn_w(1, 2)
        turn_w(1, 3)
        quant_x(4, 8)
        mm(0)
        unit(0)
        while len(summed) > 2:
            finish()
        mm(1)
        turn_w(1, 4)
        turn_w(1, 5)
        turn_w(1, 6)
        turn_w(1, 7)
        unit(1)
        while len(summed) > 2:
            finish()
        mm(2)
        unit(2)
        quant_w(1, 0)
        quant_w(1, 1)
        while len(summed) > 2:
            finish()
        mm(3)
        unit(3)
        while len(summed) > 2:
            finish()
        mm(4)
        unit(4)
        while len(summed) > 2:
            finish()
        mm(5)
        unit(5)
        while len(summed) > 2:
            finish()
        mm(6)
        unit(6)
        while len(summed) > 2:
            finish()
        mm(7)
        unit(7)
        while len(summed) > 2:
            finish()
        mm(8)
        unit(8)
        while len(summed) > 2:
            finish()
        mm(9)
        unit(9)
        while len(summed) > 2:
            finish()
        mm(10)
        unit(10)
        while len(summed) > 2:
            finish()
        mm(11)
        unit(11)
        while len(summed) > 2:
            finish()
        mm(12)
        unit(12)
        while len(summed) > 2:
            finish()
        mm(13)
        unit(13)
        while len(summed) > 2:
            finish()
        mm(14)
        unit(14)
        while len(summed) > 2:
            finish()
        mm(15)
        unit(15)
        while len(summed) > 2:
            finish()
